import numpy as np
import ml_dtypes


def mxq(x, axis, fmt="e4m3"):
    dtype, down = {"e4m3": (ml_dtypes.float8_e4m3fn, 7), "e5m2": (ml_dtypes.float8_e5m2, 14)}[fmt]
    v = np.moveaxis(np.asarray(x, np.float32).astype(ml_dtypes.bfloat16).astype(np.float64), axis, -1)
    blocks = v.reshape(v.shape[:-1] + (-1, 32))
    amax = np.abs(blocks).max(-1, keepdims=True)
    byte = np.maximum(np.where(amax > 0, np.frexp(amax)[1] - 1 + 127, 0) - down, 1)
    scale = np.exp2(byte - 127.0)
    codes = (blocks / scale).astype(np.float32).astype(dtype).astype(np.float64)
    return np.moveaxis((codes * scale).reshape(v.shape), -1, axis)


WIDE = False


def mx_kscale(k):
    if not WIDE:
        return np.ones(k)
    levels = np.array([10, -10, 5, -5, 0])
    a = np.random.permutation(np.resize(levels, k // 512 * 4)).reshape(k // 512, 4)
    idx = np.arange(k)
    return np.exp2(a[idx // 512, idx % 128 // 32])


BF16 = ml_dtypes.bfloat16


def bf(x):
    return np.asarray(x, np.float32).astype(BF16)


def f64(x):
    return np.asarray(x).astype(np.float64)


B, N, C_IN, C_OUT, H = 8, 512, 512, 512, 4
DH = C_OUT // H
LN_EPS = 1e-5


def setup_inputs():
    s = mx_kscale(C_IN)
    bound = 1.0 / np.sqrt(C_IN)
    return {
        "x": bf(np.random.standard_normal((B, N, C_IN)) * s),
        "q": bf(np.random.standard_normal((B, H, N, DH)) * 1.4),
        "k": bf(np.random.standard_normal((B, H, N, DH)) * 1.4),
        "W_v": bf(np.random.standard_normal((H, C_IN, DH)) * 2.0 * bound / s[None, :, None]),
        "conv_w": bf(np.random.uniform(-bound, bound, (C_OUT, C_IN)) / s[None, :]),
        "conv_b": bf(np.random.standard_normal(C_OUT) * 0.3),
        "ln_w": bf(1.0 + 0.1 * np.random.standard_normal(C_OUT)),
        "ln_b": bf(0.1 * np.random.standard_normal(C_OUT)),
    }


def reference(x, q, k, W_v, conv_w, conv_b, ln_w, ln_b):
    xq = mxq(f64(x), 2, "e4m3")
    v = xq[:, None] @ mxq(f64(W_v), 1, "e4m3")[None]
    s = f64(q) @ f64(k).transpose(0, 1, 3, 2) * (1.0 / np.sqrt(DH))
    e = np.exp(s - s.max(-1, keepdims=True))
    o = np.maximum((mxq(e, 3, "e4m3") @ mxq(v, 2, "e4m3")) / e.sum(-1, keepdims=True), 0.0)
    o = o.transpose(0, 2, 1, 3).reshape(B, N, C_OUT)
    proj = (xq @ mxq(f64(conv_w), 1, "e4m3").T) + f64(conv_b)
    y = o + proj
    mean = y.mean(-1, keepdims=True)
    var = y.var(-1, keepdims=True)
    return (y - mean) / np.sqrt(var + LN_EPS) * f64(ln_w) + f64(ln_b)

@@ -1,0 +1,330 @@
+import math
+from contextlib import ExitStack
+
+import concourse.mybir as mybir
+from concourse.masks import make_identity
+
+F32 = mybir.dt.float32
+BF16 = mybir.dt.bfloat16
+U32 = mybir.dt.uint32
+U8 = mybir.dt.uint8
+FP8X4 = mybir.dt.float8_e4m3fn_x4
+ALU = mybir.AluOpType
+ACT = mybir.ActivationFunctionType
+AXIS = mybir.AxisListType
+
+P = 128
+PACK = 4
+B, N, C_IN, C_OUT, H = 8, 512, 512, 512, 4
+DH = C_OUT // H
+NODE_TILES = N // P
+LN_EPS = 1e-5
+SCORE_SCALE = 1.0 / math.sqrt(DH)
+
+assert C_IN == P * PACK and N == P * PACK
+assert DH == P and NODE_TILES == PACK
+
+FLOPS = 2 * B * (N * C_IN * H * DH + N * C_IN * C_OUT + 2 * H * N * N * DH)
+
+SCORES_LAG = H
+FINISH_LAG = SCORES_LAG + 1
+
+
+def tile_transformergraphconv_pa_t_kernel(
+    tc, x, q, k, W_v, conv_w, conv_b, ln_w, ln_b, out
+):
+    nc = tc.nc
+    with ExitStack() as ctx:
+        const = ctx.enter_context(tc.tile_pool(name="const", bufs=1))
+        rows_pool = ctx.enter_context(tc.tile_pool(name="rows", bufs=2))
+        batch_pool = ctx.enter_context(tc.tile_pool(name="batch", bufs=3))
+        work = ctx.enter_context(tc.tile_pool(name="work", bufs=3))
+        small = ctx.enter_context(tc.tile_pool(name="small", bufs=4))
+        score_banks = ctx.enter_context(tc.psum_pool(name="score_banks", bufs=4))
+        flip_banks = ctx.enter_context(tc.psum_pool(name="flip_banks", bufs=2))
+        product_banks = ctx.enter_context(tc.psum_pool(name="product_banks", bufs=2))
+
+        def head_cols(h):
+            return slice(h * DH, (h + 1) * DH)
+
+        def tile_cols(j):
+            return slice(j * P, (j + 1) * P)
+
+        x_rows, q_rows, k_rows = {}, {}, {}
+
+        def load_batch(b):
+            q_tile = rows_pool.tile([P, H, NODE_TILES, DH], BF16, name="q_tile")
+            nc.sync.dma_start(
+                out=q_tile[:].rearrange("p h j d -> p h (j d)"),
+                in_=q[b].rearrange("h (p j) d -> p h (j d)", j=NODE_TILES),
+            )
+            k_tile = rows_pool.tile([P, H, NODE_TILES, DH], BF16, name="k_tile")
+            nc.sync.dma_start(
+                out=k_tile[:].rearrange("p h j d -> p h (j d)"),
+                in_=k[b].rearrange("h (p j) d -> p h (j d)", j=NODE_TILES),
+            )
+            x_tile = rows_pool.tile([P, NODE_TILES * C_IN], BF16, name="x_tile")
+            nc.sync.dma_start(
+                out=x_tile[:], in_=x[b].rearrange("(p j) c -> p (j c)", j=NODE_TILES)
+            )
+            q_rows[b], k_rows[b], x_rows[b] = q_tile, k_tile, x_tile
+
+        load_batch(0)
+
+        ident_bf16 = const.tile([P, P], BF16, name="ident_bf16")
+        make_identity(nc, ident_bf16[:])
+        ident_f32 = const.tile([P, P], F32, name="ident_f32")
+        make_identity(nc, ident_f32[:])
+        minus_half = const.tile([P, 1], F32, name="minus_half")
+        nc.vector.memset(minus_half[:], -0.5)
+
+        def quantise_channels_last(rows, codes, scales):
+            words = rows.bitcast(F32)
+            grouped = work.tile([P, PACK * P * PACK], BF16, name="grouped", align_bytes=64)
+            grouped_words = grouped[:].bitcast(F32).rearrange("p (c u) -> p c u", u=2)
+            for pair in range(2):
+                flipped = flip_banks.tile([P, 2, 2 * P], F32, name="flipped", tag="flip")
+                for i in range(2):
+                    r = 2 * pair + i
+                    for u in range(2):
+                        first_word = r * (C_IN // 2) + u * P
+                        nc.tensor.transpose(
+                            flipped[:, u, tile_cols(i)],
+                            words[:, first_word : first_word + P],
+                            ident_f32[:],
+                        )
+                nc.scalar.copy(
+                    out=grouped_words[:, pair * 2 * P : (pair + 1) * 2 * P, :],
+                    in_=flipped[:].rearrange("p u c -> p c u"),
+                )
+            nc.vector.quantize_mx(out=codes.bitcast(FP8X4), scales=scales, in_=grouped[:])
+
+        wv_rows = const.tile([P, H, PACK, DH], BF16, name="wv_rows")
+        for u in range(2):
+            nc.scalar.dma_start(
+                out=wv_rows[:, :, 2 * u : 2 * u + 2, :].rearrange("p h i d -> p h (i d)"),
+                in_=W_v[:, u * 2 * P : (u + 1) * 2 * P, :].rearrange(
+                    "h (p i) d -> p h (i d)", i=2
+                ),
+            )
+        wv_grouped = const.tile([P, H, DH, PACK], BF16, name="wv_grouped", align_bytes=64)
+        nc.vector.tensor_copy(out=wv_grouped[:], in_=wv_rows[:].rearrange("p h t d -> p h d t"))
+        wv_codes = const.tile([P, H * DH], U32, name="wv_codes", align_bytes=64)
+        wv_scales = const.tile([P, H * DH], U8, name="wv_scales", align_bytes=64)
+        nc.vector.quantize_mx(
+            out=wv_codes[:].bitcast(FP8X4),
+            scales=wv_scales[:],
+            in_=wv_grouped[:].rearrange("p h d t -> p (h d t)"),
+        )
+
+        cw_rows = const.tile([P, PACK * C_IN], BF16, name="cw_rows")
+        nc.scalar.dma_start(
+            out=cw_rows[:].rearrange("p (r c) -> p r c", c=C_IN),
+            in_=conv_w.rearrange("(r p) c -> p r c", p=P),
+        )
+        cw_codes = const.tile([P, C_OUT], U32, name="cw_codes", align_bytes=64)
+        cw_scales = const.tile([P, C_OUT], U8, name="cw_scales", align_bytes=64)
+        quantise_channels_last(cw_rows[:], cw_codes[:], cw_scales[:])
+
+        bias_all = const.tile([P, C_OUT], BF16, name="bias_all")
+        nc.scalar.dma_start(out=bias_all[:], in_=conv_b.partition_broadcast(P))
+        gain_all = const.tile([P, C_OUT], BF16, name="gain_all")
+        nc.scalar.dma_start(out=gain_all[:], in_=ln_w.partition_broadcast(P))
+        shift_all = const.tile([P, C_OUT], BF16, name="shift_all")
+        nc.scalar.dma_start(out=shift_all[:], in_=ln_b.partition_broadcast(P))
+
+        x_codes, x_scales, qk_flipped = {}, {}, {}
+        v_grouped, v_codes, v_scales = {}, {}, {}
+
+        def prepare_nodes(b):
+            xc = batch_pool.tile([P, N], U32, name="xc", align_bytes=64)
+            xs = batch_pool.tile([P, N], U8, name="xs", align_bytes=64)
+            quantise_channels_last(x_rows[b][:], xc[:], xs[:])
+            qk = batch_pool.tile([P, H, 2, N], BF16, name="qk")
+            vg = batch_pool.tile([P, H, DH, PACK], BF16, name="vg", align_bytes=64)
+            vc = batch_pool.tile([P, H * DH], U32, name="vc", align_bytes=64)
+            vs = batch_pool.tile([P, H * DH], U8, name="vs", align_bytes=64)
+            x_codes[b], x_scales[b], qk_flipped[b] = xc, xs, qk
+            v_grouped[b], v_codes[b], v_scales[b] = vg, vc, vs
+
+        def prepare_head(b, h):
+            flipped = flip_banks.tile([P, 2, N], BF16, name="flipped", tag="flip")
+            for j in range(NODE_TILES):
+                nc.tensor.transpose(flipped[:, 0, tile_cols(j)], q_rows[b][:, h, j, :], ident_bf16[:])
+                nc.tensor.transpose(flipped[:, 1, tile_cols(j)], k_rows[b][:, h, j, :], ident_bf16[:])
+            nc.scalar.copy(out=qk_flipped[b][:, h], in_=flipped[:])
+
+            values = product_banks.tile([P, PACK, DH], F32, name="values", tag="product")
+            for t in range(PACK):
+                nc.tensor.matmul_mx(
+                    out=values[:, t, :],
+                    lhsT=x_codes[b][:, tile_cols(t)].bitcast(FP8X4),
+                    lhsT_scale=x_scales[b][:, tile_cols(t)],
+                    rhs=wv_codes[:, head_cols(h)].bitcast(FP8X4),
+                    rhs_scale=wv_scales[:, head_cols(h)],
+                    start=True,
+                    stop=True,
+                )
+            nc.scalar.copy(out=v_grouped[b][:, h], in_=values[:].rearrange("p t d -> p d t"))
+            nc.vector.quantize_mx(
+                out=v_codes[b][:, head_cols(h)].bitcast(FP8X4),
+                scales=v_scales[b][:, head_cols(h)],
+                in_=v_grouped[b][:, h].rearrange("p d t -> p (d t)"),
+            )
+
+        e_rows, row_sums = {}, {}
+
+        def scores_and_exp(b, j):
+            row_max = small.tile([P, H], F32, name="row_max")
+            scores = []
+            for h in range(H):
+                s = score_banks.tile([P, N], F32, name="s", tag="scores")
+                nc.tensor.matmul(
+                    out=s[:],
+                    lhsT=qk_flipped[b][:, h, 0, tile_cols(j)],
+                    rhs=qk_flipped[b][:, h, 1, :],
+                    start=True,
+                    stop=True,
+                )
+                nc.vector.tensor_reduce(out=row_max[:, h : h + 1], in_=s[:], axis=AXIS.X, op=ALU.max)
+                scores.append(s)
+            exp_bias = small.tile([P, H], F32, name="exp_bias")
+            nc.vector.tensor_scalar(
+                out=exp_bias[:], in0=row_max[:], scalar1=-SCORE_SCALE, scalar2=None, op0=ALU.mult
+            )
+            e_tile = work.tile([P, H, N], BF16, name="e_tile")
+            row_sum = small.tile([P, H], F32, name="row_sum")
+            for h in range(H):
+                nc.scalar.activation(
+                    out=e_tile[:, h, :],
+                    in_=scores[h][:],
+                    func=ACT.Exp,
+                    bias=exp_bias[:, h : h + 1],
+                    scale=SCORE_SCALE,
+                    accum_out=row_sum[:, h : h + 1],
+                )
+            e_rows[(b, j)], row_sums[(b, j)] = e_tile, row_sum
+
+        def finish_tile(b, j):
+            e_tile = e_rows[(b, j)]
+            e_grouped = work.tile([P, H, P, PACK], BF16, name="e_grouped", align_bytes=64)
+            for pair in range(H // 2):
+                flipped = flip_banks.tile([P, 2, PACK, P], BF16, name="flipped", tag="flip")
+                for i in range(2):
+                    for t in range(PACK):
+                        nc.tensor.transpose(
+                            flipped[:, i, t, :], e_tile[:, 2 * pair + i, tile_cols(t)], ident_bf16[:]
+                        )
+                nc.scalar.copy(
+                    out=e_grouped[:, 2 * pair : 2 * pair + 2],
+                    in_=flipped[:].rearrange("p i t n -> p i n t"),
+                )
+            e_codes = work.tile([P, H * P], U32, name="e_codes", align_bytes=64)
+            e_scales = work.tile([P, H * P], U8, name="e_scales", align_bytes=64)
+            nc.vector.quantize_mx(
+                out=e_codes[:].bitcast(FP8X4),
+                scales=e_scales[:],
+                in_=e_grouped[:].rearrange("p h n t -> p (h n t)"),
+            )
+
+            attended = product_banks.tile([P, H, DH], F32, name="attended", tag="product")
+            for h in range(H):
+                nc.tensor.matmul_mx(
+                    out=attended[:, h, :],
+                    lhsT=e_codes[:, tile_cols(h)].bitcast(FP8X4),
+                    lhsT_scale=e_scales[:, tile_cols(h)],
+                    rhs=v_codes[b][:, head_cols(h)].bitcast(FP8X4),
+                    rhs_scale=v_scales[b][:, head_cols(h)],
+                    start=True,
+                    stop=True,
+                )
+            projected = product_banks.tile([P, C_OUT], F32, name="projected", tag="product")
+            nc.tensor.matmul_mx(
+                out=projected[:],
+                lhsT=x_codes[b][:, tile_cols(j)].bitcast(FP8X4),
+                lhsT_scale=x_scales[b][:, tile_cols(j)],
+                rhs=cw_codes[:].bitcast(FP8X4),
+                rhs_scale=cw_scales[:],
+                start=True,
+                stop=True,
+            )
+
+            inv_sum = small.tile([P, H], F32, name="inv_sum")
+            nc.vector.reciprocal(inv_sum[:], row_sums[(b, j)][:])
+            conv = work.tile([P, C_OUT], F32, name="conv")
+            nc.vector.tensor_tensor(out=conv[:], in0=projected[:], in1=bias_all[:], op=ALU.add)
+            mixed = work.tile([P, H, DH], F32, name="mixed")
+            nc.vector.tensor_tensor(
+                out=mixed[:],
+                in0=attended[:],
+                in1=inv_sum[:].unsqueeze(2).to_broadcast([P, H, DH]),
+                op=ALU.mult,
+            )
+            y = work.tile([P, C_OUT], F32, name="y")
+            y_sum = small.tile([P, 1], F32, name="y_sum")
+            nc.vector.scalar_tensor_tensor(
+                out=y[:],
+                in0=mixed[:].rearrange("p h d -> p (h d)"),
+                scalar=0.0,
+                in1=conv[:],
+                op0=ALU.max,
+                op1=ALU.add,
+                accum_out=y_sum[:],
+            )
+
+            neg_mean = small.tile([P, 1], F32, name="neg_mean")
+            nc.vector.tensor_scalar(
+                out=neg_mean[:], in0=y_sum[:], scalar1=-1.0 / C_OUT, scalar2=None, op0=ALU.mult
+            )
+            squares = work.tile([P, C_OUT], BF16, name="squares")
+            square_sum = small.tile([P, 1], F32, name="square_sum")
+            nc.scalar.activation(
+                out=squares[:],
+                in_=y[:],
+                func=ACT.Square,
+                bias=neg_mean[:],
+                scale=1.0,
+                accum_out=square_sum[:],
+            )
+            var_eps = small.tile([P, 1], F32, name="var_eps")
+            nc.gpsimd.tensor_scalar(
+                out=var_eps[:],
+                in0=square_sum[:],
+                scalar1=1.0 / C_OUT,
+                scalar2=LN_EPS,
+                op0=ALU.mult,
+                op1=ALU.add,
+            )
+            inv_std = small.tile([P, 1], F32, name="inv_std")
+            nc.gpsimd.tensor_tensor(out=inv_std[:], in0=var_eps[:], in1=minus_half[:], op=ALU.pow)
+
+            centred = work.tile([P, C_OUT], F32, name="centred")
+            nc.vector.scalar_tensor_tensor(
+                out=centred[:], in0=y[:], scalar=neg_mean[:], in1=gain_all[:], op0=ALU.add, op1=ALU.mult
+            )
+            result = work.tile([P, C_OUT], F32, name="result")
+            nc.vector.scalar_tensor_tensor(
+                out=result[:],
+                in0=centred[:],
+                scalar=inv_std[:],
+                in1=shift_all[:],
+                op0=ALU.mult,
+                op1=ALU.add,
+            )
+            nc.sync.dma_start(
+                out=out[b].rearrange("(p j) c -> p j c", j=NODE_TILES)[:, j, :], in_=result[:]
+            )
+
+        steps = B * H
+        for step in range(steps + FINISH_LAG):
+            if step < steps:
+                b, h = divmod(step, H)
+                if h == 0:
+                    if b + 1 < B:
+                        load_batch(b + 1)
+                    prepare_nodes(b)
+                prepare_head(b, h)
+            if 0 <= step - SCORES_LAG < steps:
+                scores_and_exp(*divmod(step - SCORES_LAG, NODE_TILES))
+            if 0 <= step - FINISH_LAG < steps:
+                finish_tile(*divmod(step - FINISH_LAG, NODE_TILES))

@@ -26,8 +26,16 @@ assert DH == P and NODE_TILES == PACK
 
 FLOPS = 2 * B * (N * C_IN * H * DH + N * C_IN * C_OUT + 2 * H * N * N * DH)
 
-SCORES_LAG = H
-FINISH_LAG = SCORES_LAG + 1
+ITEMS = B * NODE_TILES * H
+TILES = B * NODE_TILES
+HEADS = B * H
+
+QK_LEAD = 4
+VALUES_LEAD = 3
+NODES_LEAD = 4
+LOAD_LEAD = 8
+FIRST_STEP = -H * LOAD_LEAD
+LAST_STEP = ITEMS + 3 * H
 
 
 def tile_transformergraphconv_pa_t_kernel(
@@ -35,14 +43,15 @@ def tile_transformergraphconv_pa_t_kernel(
 ):
     nc = tc.nc
     with ExitStack() as ctx:
+        ctx.enter_context(tc.manual_schedule())
         const = ctx.enter_context(tc.tile_pool(name="const", bufs=1))
         rows_pool = ctx.enter_context(tc.tile_pool(name="rows", bufs=2))
         batch_pool = ctx.enter_context(tc.tile_pool(name="batch", bufs=3))
         work = ctx.enter_context(tc.tile_pool(name="work", bufs=3))
         small = ctx.enter_context(tc.tile_pool(name="small", bufs=4))
-        score_banks = ctx.enter_context(tc.psum_pool(name="score_banks", bufs=4))
+        score_banks = ctx.enter_context(tc.psum_pool(name="score_banks", bufs=3))
         flip_banks = ctx.enter_context(tc.psum_pool(name="flip_banks", bufs=2))
-        product_banks = ctx.enter_context(tc.psum_pool(name="product_banks", bufs=2))
+        product_banks = ctx.enter_context(tc.psum_pool(name="product_banks", bufs=3))
 
         def head_cols(h):
             return slice(h * DH, (h + 1) * DH)
@@ -69,25 +78,15 @@ def tile_transformergraphconv_pa_t_kernel(
             )
             q_rows[b], k_rows[b], x_rows[b] = q_tile, k_tile, x_tile
 
-        load_batch(0)
-
-        ident_bf16 = const.tile([P, P], BF16, name="ident_bf16")
-        make_identity(nc, ident_bf16[:])
-        ident_f32 = const.tile([P, P], F32, name="ident_f32")
-        make_identity(nc, ident_f32[:])
-        minus_half = const.tile([P, 1], F32, name="minus_half")
-        nc.vector.memset(minus_half[:], -0.5)
-
-        def quantise_channels_last(rows, codes, scales):
+        def flip_channels(rows):
             words = rows.bitcast(F32)
             grouped = work.tile([P, PACK * P * PACK], BF16, name="grouped", align_bytes=64)
             grouped_words = grouped[:].bitcast(F32).rearrange("p (c u) -> p c u", u=2)
             for pair in range(2):
                 flipped = flip_banks.tile([P, 2, 2 * P], F32, name="flipped", tag="flip")
                 for i in range(2):
-                    r = 2 * pair + i
                     for u in range(2):
-                        first_word = r * (C_IN // 2) + u * P
+                        first_word = (2 * pair + i) * (C_IN // 2) + u * P
                         nc.tensor.transpose(
                             flipped[:, u, tile_cols(i)],
                             words[:, first_word : first_word + P],
@@ -97,8 +96,13 @@ def tile_transformergraphconv_pa_t_kernel(
                     out=grouped_words[:, pair * 2 * P : (pair + 1) * 2 * P, :],
                     in_=flipped[:].rearrange("p u c -> p c u"),
                 )
-            nc.vector.quantize_mx(out=codes.bitcast(FP8X4), scales=scales, in_=grouped[:])
+            return grouped
 
+        cw_rows = const.tile([P, PACK * C_IN], BF16, name="cw_rows")
+        nc.scalar.dma_start(
+            out=cw_rows[:].rearrange("p (r c) -> p r c", c=C_IN),
+            in_=conv_w.rearrange("(r p) c -> p r c", p=P),
+        )
         wv_rows = const.tile([P, H, PACK, DH], BF16, name="wv_rows")
         for u in range(2):
             nc.scalar.dma_start(
@@ -107,6 +111,26 @@ def tile_transformergraphconv_pa_t_kernel(
                     "h (p i) d -> p h (i d)", i=2
                 ),
             )
+        bias_all = const.tile([P, C_OUT], BF16, name="bias_all")
+        nc.scalar.dma_start(out=bias_all[:], in_=conv_b.partition_broadcast(P))
+        gain_all = const.tile([P, C_OUT], BF16, name="gain_all")
+        nc.scalar.dma_start(out=gain_all[:], in_=ln_w.partition_broadcast(P))
+        shift_all = const.tile([P, C_OUT], BF16, name="shift_all")
+        nc.scalar.dma_start(out=shift_all[:], in_=ln_b.partition_broadcast(P))
+
+        ident_f32 = const.tile([P, P], F32, name="ident_f32")
+        make_identity(nc, ident_f32[:])
+        ident_bf16 = const.tile([P, P], BF16, name="ident_bf16")
+        make_identity(nc, ident_bf16[:])
+        minus_half = const.tile([P, 1], F32, name="minus_half")
+        nc.vector.memset(minus_half[:], -0.5)
+
+        cw_grouped = flip_channels(cw_rows[:])
+        cw_codes = const.tile([P, C_OUT], U32, name="cw_codes", align_bytes=64)
+        cw_scales = const.tile([P, C_OUT], U8, name="cw_scales", align_bytes=64)
+        nc.vector.quantize_mx(
+            out=cw_codes[:].bitcast(FP8X4), scales=cw_scales[:], in_=cw_grouped[:]
+        )
         wv_grouped = const.tile([P, H, DH, PACK], BF16, name="wv_grouped", align_bytes=64)
         nc.vector.tensor_copy(out=wv_grouped[:], in_=wv_rows[:].rearrange("p h t d -> p h d t"))
         wv_codes = const.tile([P, H * DH], U32, name="wv_codes", align_bytes=64)
@@ -117,43 +141,30 @@ def tile_transformergraphconv_pa_t_kernel(
             in_=wv_grouped[:].rearrange("p h d t -> p (h d t)"),
         )
 
-        cw_rows = const.tile([P, PACK * C_IN], BF16, name="cw_rows")
-        nc.scalar.dma_start(
-            out=cw_rows[:].rearrange("p (r c) -> p r c", c=C_IN),
-            in_=conv_w.rearrange("(r p) c -> p r c", p=P),
-        )
-        cw_codes = const.tile([P, C_OUT], U32, name="cw_codes", align_bytes=64)
-        cw_scales = const.tile([P, C_OUT], U8, name="cw_scales", align_bytes=64)
-        quantise_channels_last(cw_rows[:], cw_codes[:], cw_scales[:])
+        x_grouped, x_codes, x_scales = {}, {}, {}
 
-        bias_all = const.tile([P, C_OUT], BF16, name="bias_all")
-        nc.scalar.dma_start(out=bias_all[:], in_=conv_b.partition_broadcast(P))
-        gain_all = const.tile([P, C_OUT], BF16, name="gain_all")
-        nc.scalar.dma_start(out=gain_all[:], in_=ln_w.partition_broadcast(P))
-        shift_all = const.tile([P, C_OUT], BF16, name="shift_all")
-        nc.scalar.dma_start(out=shift_all[:], in_=ln_b.partition_broadcast(P))
+        def flip_nodes(b):
+            x_grouped[b] = flip_channels(x_rows[b][:])
 
-        x_codes, x_scales, qk_flipped = {}, {}, {}
-        v_grouped, v_codes, v_scales = {}, {}, {}
-
-        def prepare_nodes(b):
+        def quantise_nodes(b):
             xc = batch_pool.tile([P, N], U32, name="xc", align_bytes=64)
             xs = batch_pool.tile([P, N], U8, name="xs", align_bytes=64)
-            quantise_channels_last(x_rows[b][:], xc[:], xs[:])
-            qk = batch_pool.tile([P, H, 2, N], BF16, name="qk")
-            vg = batch_pool.tile([P, H, DH, PACK], BF16, name="vg", align_bytes=64)
-            vc = batch_pool.tile([P, H * DH], U32, name="vc", align_bytes=64)
-            vs = batch_pool.tile([P, H * DH], U8, name="vs", align_bytes=64)
-            x_codes[b], x_scales[b], qk_flipped[b] = xc, xs, qk
-            v_grouped[b], v_codes[b], v_scales[b] = vg, vc, vs
+            nc.vector.quantize_mx(out=xc[:].bitcast(FP8X4), scales=xs[:], in_=x_grouped[b][:])
+            x_codes[b], x_scales[b] = xc, xs
 
-        def prepare_head(b, h):
+        qk_flipped = {}
+        value_banks, v_grouped, v_codes, v_scales = {}, {}, {}, {}
+
+        def flip_queries_and_keys(b, h):
             flipped = flip_banks.tile([P, 2, N], BF16, name="flipped", tag="flip")
             for j in range(NODE_TILES):
                 nc.tensor.transpose(flipped[:, 0, tile_cols(j)], q_rows[b][:, h, j, :], ident_bf16[:])
                 nc.tensor.transpose(flipped[:, 1, tile_cols(j)], k_rows[b][:, h, j, :], ident_bf16[:])
-            nc.scalar.copy(out=qk_flipped[b][:, h], in_=flipped[:])
+            qk = batch_pool.tile([P, 2, N], BF16, name="qk", bufs=3 * H)
+            nc.scalar.copy(out=qk[:], in_=flipped[:])
+            qk_flipped[(b, h)] = qk
 
+        def multiply_values(b, h):
             values = product_banks.tile([P, PACK, DH], F32, name="values", tag="product")
             for t in range(PACK):
                 nc.tensor.matmul_mx(
@@ -165,82 +176,94 @@ def tile_transformergraphconv_pa_t_kernel(
                     start=True,
                     stop=True,
                 )
-            nc.scalar.copy(out=v_grouped[b][:, h], in_=values[:].rearrange("p t d -> p d t"))
+            value_banks[(b, h)] = values
+
+        def round_values(b, h):
+            vg = work.tile([P, DH, PACK], BF16, name="vg", align_bytes=64)
+            nc.scalar.copy(out=vg[:], in_=value_banks[(b, h)][:].rearrange("p t d -> p d t"))
+            v_grouped[(b, h)] = vg
+
+        def quantise_values(b, h):
+            vc = batch_pool.tile([P, DH], U32, name="vc", align_bytes=64, bufs=3 * H)
+            vs = batch_pool.tile([P, DH], U8, name="vs", align_bytes=64, bufs=3 * H)
             nc.vector.quantize_mx(
-                out=v_codes[b][:, head_cols(h)].bitcast(FP8X4),
-                scales=v_scales[b][:, head_cols(h)],
-                in_=v_grouped[b][:, h].rearrange("p d t -> p (d t)"),
+                out=vc[:].bitcast(FP8X4),
+                scales=vs[:],
+                in_=v_grouped[(b, h)][:].rearrange("p d t -> p (d t)"),
             )
+            v_codes[(b, h)], v_scales[(b, h)] = vc, vs
 
-        e_rows, row_sums = {}, {}
+        scores, row_max, exp_bias, e_rows = {}, {}, {}, {}
+        row_sums, e_grouped = {}, {}
 
-        def scores_and_exp(b, j):
-            row_max = small.tile([P, H], F32, name="row_max")
-            scores = []
-            for h in range(H):
-                s = score_banks.tile([P, N], F32, name="s", tag="scores")
-                nc.tensor.matmul(
-                    out=s[:],
-                    lhsT=qk_flipped[b][:, h, 0, tile_cols(j)],
-                    rhs=qk_flipped[b][:, h, 1, :],
-                    start=True,
-                    stop=True,
-                )
-                nc.vector.tensor_reduce(out=row_max[:, h : h + 1], in_=s[:], axis=AXIS.X, op=ALU.max)
-                scores.append(s)
-            exp_bias = small.tile([P, H], F32, name="exp_bias")
+        def multiply_scores(b, j, h):
+            s = score_banks.tile([P, N], F32, name="s", tag="scores")
+            nc.tensor.matmul(
+                out=s[:],
+                lhsT=qk_flipped[(b, h)][:, 0, tile_cols(j)],
+                rhs=qk_flipped[(b, h)][:, 1, :],
+                start=True,
+                stop=True,
+            )
+            scores[(b, j, h)] = s
+
+        def find_row_maximum(b, j, h):
+            top = small.tile([P, 1], F32, name="top")
+            nc.vector.tensor_reduce(out=top[:], in_=scores[(b, j, h)][:], axis=AXIS.X, op=ALU.max)
+            row_max[(b, j, h)] = top
+
+        def scale_row_maximum(b, j, h):
+            shift = small.tile([P, 1], F32, name="shift")
             nc.vector.tensor_scalar(
-                out=exp_bias[:], in0=row_max[:], scalar1=-SCORE_SCALE, scalar2=None, op0=ALU.mult
+                out=shift[:],
+                in0=row_max[(b, j, h)][:],
+                scalar1=-SCORE_SCALE,
+                scalar2=None,
+                op0=ALU.mult,
             )
-            e_tile = work.tile([P, H, N], BF16, name="e_tile")
-            row_sum = small.tile([P, H], F32, name="row_sum")
-            for h in range(H):
-                nc.scalar.activation(
-                    out=e_tile[:, h, :],
-                    in_=scores[h][:],
-                    func=ACT.Exp,
-                    bias=exp_bias[:, h : h + 1],
-                    scale=SCORE_SCALE,
-                    accum_out=row_sum[:, h : h + 1],
-                )
-            e_rows[(b, j)], row_sums[(b, j)] = e_tile, row_sum
+            exp_bias[(b, j, h)] = shift
 
-        def finish_tile(b, j):
-            e_tile = e_rows[(b, j)]
-            e_grouped = work.tile([P, H, P, PACK], BF16, name="e_grouped", align_bytes=64)
-            for pair in range(H // 2):
-                flipped = flip_banks.tile([P, 2, PACK, P], BF16, name="flipped", tag="flip")
-                for i in range(2):
-                    for t in range(PACK):
-                        nc.tensor.transpose(
-                            flipped[:, i, t, :], e_tile[:, 2 * pair + i, tile_cols(t)], ident_bf16[:]
-                        )
-                nc.scalar.copy(
-                    out=e_grouped[:, 2 * pair : 2 * pair + 2],
-                    in_=flipped[:].rearrange("p i t n -> p i n t"),
-                )
-            e_codes = work.tile([P, H * P], U32, name="e_codes", align_bytes=64)
-            e_scales = work.tile([P, H * P], U8, name="e_scales", align_bytes=64)
+        def exponentiate(b, j, h):
+            if h == 0:
+                row_sum = small.tile([P, H], F32, name="row_sum")
+                row_sums[(b, j)] = row_sum
+            e_item = work.tile([P, N], BF16, name="e_item")
+            nc.scalar.activation(
+                out=e_item[:],
+                in_=scores[(b, j, h)][:],
+                func=ACT.Exp,
+                bias=exp_bias[(b, j, h)][:],
+                scale=SCORE_SCALE,
+                accum_out=row_sums[(b, j)][:, h : h + 1],
+            )
+            e_rows[(b, j, h)] = e_item
+
+        def flip_weights(b, j, h):
+            if h == 0:
+                eg = work.tile([P, H, P, PACK], BF16, name="eg", align_bytes=64)
+                e_grouped[(b, j)] = eg
+            flipped = flip_banks.tile([P, PACK, P], BF16, name="flipped", tag="flip")
+            for t in range(PACK):
+                nc.tensor.transpose(flipped[:, t, :], e_rows[(b, j, h)][:, tile_cols(t)], ident_bf16[:])
+            nc.scalar.copy(out=e_grouped[(b, j)][:, h], in_=flipped[:].rearrange("p t n -> p n t"))
+
+        e_codes, e_scales, attended, projected = {}, {}, {}, {}
+        inv_sums, conv, mixed, y_tiles, neg_means, inv_stds, centred = {}, {}, {}, {}, {}, {}, {}
+
+        def quantise_weights(b, j):
+            ec = work.tile([P, H * P], U32, name="ec", align_bytes=64)
+            es = work.tile([P, H * P], U8, name="es", align_bytes=64)
             nc.vector.quantize_mx(
-                out=e_codes[:].bitcast(FP8X4),
-                scales=e_scales[:],
-                in_=e_grouped[:].rearrange("p h n t -> p (h n t)"),
+                out=ec[:].bitcast(FP8X4),
+                scales=es[:],
+                in_=e_grouped[(b, j)][:].rearrange("p h n t -> p (h n t)"),
             )
+            e_codes[(b, j)], e_scales[(b, j)] = ec, es
 
-            attended = product_banks.tile([P, H, DH], F32, name="attended", tag="product")
-            for h in range(H):
-                nc.tensor.matmul_mx(
-                    out=attended[:, h, :],
-                    lhsT=e_codes[:, tile_cols(h)].bitcast(FP8X4),
-                    lhsT_scale=e_scales[:, tile_cols(h)],
-                    rhs=v_codes[b][:, head_cols(h)].bitcast(FP8X4),
-                    rhs_scale=v_scales[b][:, head_cols(h)],
-                    start=True,
-                    stop=True,
-                )
-            projected = product_banks.tile([P, C_OUT], F32, name="projected", tag="product")
+        def multiply_projection(b, j):
+            proj = product_banks.tile([P, C_OUT], F32, name="proj", tag="product")
             nc.tensor.matmul_mx(
-                out=projected[:],
+                out=proj[:],
                 lhsT=x_codes[b][:, tile_cols(j)].bitcast(FP8X4),
                 lhsT_scale=x_scales[b][:, tile_cols(j)],
                 rhs=cw_codes[:].bitcast(FP8X4),
@@ -248,41 +271,77 @@ def tile_transformergraphconv_pa_t_kernel(
                 start=True,
                 stop=True,
             )
+            projected[(b, j)] = proj
 
+        def multiply_weights_and_values(b, j):
+            att = product_banks.tile([P, H, DH], F32, name="att", tag="product")
+            for h in range(H):
+                nc.tensor.matmul_mx(
+                    out=att[:, h, :],
+                    lhsT=e_codes[(b, j)][:, tile_cols(h)].bitcast(FP8X4),
+                    lhsT_scale=e_scales[(b, j)][:, tile_cols(h)],
+                    rhs=v_codes[(b, h)][:].bitcast(FP8X4),
+                    rhs_scale=v_scales[(b, h)][:],
+                    start=True,
+                    stop=True,
+                )
+            attended[(b, j)] = att
+
+        def invert_row_sums(b, j):
             inv_sum = small.tile([P, H], F32, name="inv_sum")
             nc.vector.reciprocal(inv_sum[:], row_sums[(b, j)][:])
-            conv = work.tile([P, C_OUT], F32, name="conv")
-            nc.vector.tensor_tensor(out=conv[:], in0=projected[:], in1=bias_all[:], op=ALU.add)
-            mixed = work.tile([P, H, DH], F32, name="mixed")
+            inv_sums[(b, j)] = inv_sum
+
+        def add_conv_bias(b, j):
+            cv = work.tile([P, C_OUT], F32, name="cv")
+            nc.vector.tensor_tensor(out=cv[:], in0=projected[(b, j)][:], in1=bias_all[:], op=ALU.add)
+            conv[(b, j)] = cv
+
+        def divide_by_row_sums(b, j):
+            scaled = work.tile([P, H, DH], F32, name="scaled")
             nc.vector.tensor_tensor(
-                out=mixed[:],
-                in0=attended[:],
-                in1=inv_sum[:].unsqueeze(2).to_broadcast([P, H, DH]),
+                out=scaled[:],
+                in0=attended[(b, j)][:],
+                in1=inv_sums[(b, j)][:].unsqueeze(2).to_broadcast([P, H, DH]),
                 op=ALU.mult,
             )
+            mixed[(b, j)] = scaled
+
+        y_sums = {}
+
+        def add_streams(b, j):
             y = work.tile([P, C_OUT], F32, name="y")
             y_sum = small.tile([P, 1], F32, name="y_sum")
             nc.vector.scalar_tensor_tensor(
                 out=y[:],
-                in0=mixed[:].rearrange("p h d -> p (h d)"),
+                in0=mixed[(b, j)][:].rearrange("p h d -> p (h d)"),
                 scalar=0.0,
-                in1=conv[:],
+                in1=conv[(b, j)][:],
                 op0=ALU.max,
                 op1=ALU.add,
                 accum_out=y_sum[:],
             )
+            y_tiles[(b, j)], y_sums[(b, j)] = y, y_sum
 
+        def negate_mean(b, j):
             neg_mean = small.tile([P, 1], F32, name="neg_mean")
             nc.vector.tensor_scalar(
-                out=neg_mean[:], in0=y_sum[:], scalar1=-1.0 / C_OUT, scalar2=None, op0=ALU.mult
+                out=neg_mean[:],
+                in0=y_sums[(b, j)][:],
+                scalar1=-1.0 / C_OUT,
+                scalar2=None,
+                op0=ALU.mult,
             )
+            neg_means[(b, j)] = neg_mean
+
+        def invert_deviation(b, j):
             squares = work.tile([P, C_OUT], BF16, name="squares")
             square_sum = small.tile([P, 1], F32, name="square_sum")
             nc.scalar.activation(
                 out=squares[:],
-                in_=y[:],
+                in_=y_tiles[(b, j)][:],
                 func=ACT.Square,
-                bias=neg_mean[:],
+                bias=neg_means[(b, j)][:],
                 scale=1.0,
                 accum_out=square_sum[:],
             )
@@ -297,16 +356,26 @@ def tile_transformergraphconv_pa_t_kernel(
             )
             inv_std = small.tile([P, 1], F32, name="inv_std")
             nc.gpsimd.tensor_tensor(out=inv_std[:], in0=var_eps[:], in1=minus_half[:], op=ALU.pow)
+            inv_stds[(b, j)] = inv_std
 
-            centred = work.tile([P, C_OUT], F32, name="centred")
+        def centre_and_gain(b, j):
+            ct = work.tile([P, C_OUT], F32, name="ct")
             nc.vector.scalar_tensor_tensor(
-                out=centred[:], in0=y[:], scalar=neg_mean[:], in1=gain_all[:], op0=ALU.add, op1=ALU.mult
+                out=ct[:],
+                in0=y_tiles[(b, j)][:],
+                scalar=neg_means[(b, j)][:],
+                in1=gain_all[:],
+                op0=ALU.add,
+                op1=ALU.mult,
             )
+            centred[(b, j)] = ct
+
+        def normalise_and_store(b, j):
             result = work.tile([P, C_OUT], F32, name="result")
             nc.vector.scalar_tensor_tensor(
                 out=result[:],
-                in0=centred[:],
-                scalar=inv_std[:],
+                in0=centred[(b, j)][:],
+                scalar=inv_stds[(b, j)][:],
                 in1=shift_all[:],
                 op0=ALU.mult,
                 op1=ALU.add,
@@ -315,16 +384,77 @@ def tile_transformergraphconv_pa_t_kernel(
                 out=out[b].rearrange("(p j) c -> p j c", j=NODE_TILES)[:, j, :], in_=result[:]
             )
 
-        steps = B * H
-        for step in range(steps + FINISH_LAG):
-            if step < steps:
-                b, h = divmod(step, H)
-                if h == 0:
-                    if b + 1 < B:
-                        load_batch(b + 1)
-                    prepare_nodes(b)
-                prepare_head(b, h)
-            if 0 <= step - SCORES_LAG < steps:
-                scores_and_exp(*divmod(step - SCORES_LAG, NODE_TILES))
-            if 0 <= step - FINISH_LAG < steps:
-                finish_tile(*divmod(step - FINISH_LAG, NODE_TILES))
+        def item(i):
+            b, rest = divmod(i, NODE_TILES * H)
+            j, h = divmod(rest, H)
+            return b, j, h
+
+        def is_item(i):
+            return 0 <= i < ITEMS
+
+        def is_tile(n):
+            return 0 <= n < TILES
+
+        def is_head(m):
+            return 0 <= m < HEADS
+
+        def batch_starting_at(n):
+            if is_tile(n) and n % NODE_TILES == 0:
+                return n // NODE_TILES
+            return None
+
+        for step in range(FIRST_STEP, LAST_STEP):
+            turn, part = divmod(step, H)
+
+            if is_item(step):
+                multiply_scores(*item(step))
+            if is_item(step - 1):
+                find_row_maximum(*item(step - 1))
+            if is_item(step - 2):
+                exponentiate(*item(step - 2))
+            if is_item(step - 3):
+                flip_weights(*item(step - 3))
+
+            done = divmod(turn - 2, NODE_TILES)
+            if part == 0:
+                if batch_starting_at(turn + LOAD_LEAD) is not None:
+                    load_batch(batch_starting_at(turn + LOAD_LEAD))
+                if is_head(turn - 1 + VALUES_LEAD):
+                    round_values(*divmod(turn - 1 + VALUES_LEAD, H))
+                if is_tile(turn - 2):
+                    invert_row_sums(*done)
+                    add_conv_bias(*done)
+            if part == 1 and is_tile(turn - 2):
+                add_streams(*done)
+            if part == 2 and is_tile(turn - 2):
+                centre_and_gain(*done)
+            if part == 3:
+                if batch_starting_at(turn - 1 + NODES_LEAD) is not None:
+                    quantise_nodes(batch_starting_at(turn - 1 + NODES_LEAD))
+                if is_tile(turn - 1):
+                    quantise_weights(*divmod(turn - 1, NODE_TILES))
+
+            if is_item(step - 1):
+                scale_row_maximum(*item(step - 1))
+
+            if part == 0 and is_tile(turn - 2):
+                divide_by_row_sums(*done)
+            if part == 1:
+                if is_tile(turn - 2):
+                    negate_mean(*done)
+                    invert_deviation(*done)
+                if is_head(turn - 1 + VALUES_LEAD):
+                    quantise_values(*divmod(turn - 1 + VALUES_LEAD, H))
+            if part == 2:
+                if is_tile(turn - 3):
+                    normalise_and_store(*divmod(turn - 3, NODE_TILES))
+                if is_head(turn + QK_LEAD):
+                    flip_queries_and_keys(*divmod(turn + QK_LEAD, H))
+            if part == 3:
+                if is_tile(turn - 1):
+                    multiply_projection(*divmod(turn - 1, NODE_TILES))
+                    multiply_weights_and_values(*divmod(turn - 1, NODE_TILES))
+                if is_head(turn + VALUES_LEAD):
+                    multiply_values(*divmod(turn + VALUES_LEAD, H))
+                if batch_starting_at(turn + NODES_LEAD) is not None:
+                    flip_nodes(batch_starting_at(turn + NODES_LEAD))

@@ -35,7 +35,8 @@ VALUES_LEAD = 3
 NODES_LEAD = 4
 LOAD_LEAD = 8
 FIRST_STEP = -H * LOAD_LEAD
-LAST_STEP = ITEMS + 3 * H
+FINISH_LAG = 2
+LAST_STEP = H * (TILES - 1 + FINISH_LAG) + 2
 
 
 def tile_transformergraphconv_pa_t_kernel(
@@ -152,7 +153,7 @@ def tile_transformergraphconv_pa_t_kernel(
             nc.vector.quantize_mx(out=xc[:].bitcast(FP8X4), scales=xs[:], in_=x_grouped[b][:])
             x_codes[b], x_scales[b] = xc, xs
 
-        qk_flipped = {}
+        qk_banks, qk_flipped = {}, {}
         value_banks, v_grouped, v_codes, v_scales = {}, {}, {}, {}
 
         def flip_queries_and_keys(b, h):
@@ -160,8 +161,11 @@ def tile_transformergraphconv_pa_t_kernel(
             for j in range(NODE_TILES):
                 nc.tensor.transpose(flipped[:, 0, tile_cols(j)], q_rows[b][:, h, j, :], ident_bf16[:])
                 nc.tensor.transpose(flipped[:, 1, tile_cols(j)], k_rows[b][:, h, j, :], ident_bf16[:])
+            qk_banks[(b, h)] = flipped
+
+        def keep_queries_and_keys(b, h):
             qk = batch_pool.tile([P, 2, N], BF16, name="qk", bufs=3 * H)
-            nc.scalar.copy(out=qk[:], in_=flipped[:])
+            nc.vector.tensor_copy(out=qk[:], in_=qk_banks[(b, h)][:])
             qk_flipped[(b, h)] = qk
 
         def multiply_values(b, h):
@@ -248,7 +252,7 @@ def tile_transformergraphconv_pa_t_kernel(
             nc.scalar.copy(out=e_grouped[(b, j)][:, h], in_=flipped[:].rearrange("p t n -> p n t"))
 
         e_codes, e_scales, attended, projected = {}, {}, {}, {}
-        inv_sums, conv, mixed, y_tiles, neg_means, inv_stds, centred = {}, {}, {}, {}, {}, {}, {}
+        inv_sums, conv, mixed, y_tiles, neg_means, inv_stds = {}, {}, {}, {}, {}, {}
 
         def quantise_weights(b, j):
             ec = work.tile([P, H * P], U32, name="ec", align_bytes=64)
@@ -358,28 +362,20 @@ def tile_transformergraphconv_pa_t_kernel(
             nc.gpsimd.tensor_tensor(out=inv_std[:], in0=var_eps[:], in1=minus_half[:], op=ALU.pow)
             inv_stds[(b, j)] = inv_std
 
-        def centre_and_gain(b, j):
-            ct = work.tile([P, C_OUT], F32, name="ct")
-            nc.vector.scalar_tensor_tensor(
-                out=ct[:],
+        def normalise_and_store(b, j):
+            z = work.tile([P, C_OUT], F32, name="z")
+            nc.gpsimd.tensor_scalar(
+                out=z[:],
                 in0=y_tiles[(b, j)][:],
-                scalar=neg_means[(b, j)][:],
-                in1=gain_all[:],
+                scalar1=neg_means[(b, j)][:],
+                scalar2=inv_stds[(b, j)][:],
                 op0=ALU.add,
                 op1=ALU.mult,
             )
-            centred[(b, j)] = ct
-
-        def normalise_and_store(b, j):
+            gained = work.tile([P, C_OUT], F32, name="gained")
+            nc.gpsimd.tensor_tensor(out=gained[:], in0=z[:], in1=gain_all[:], op=ALU.mult)
             result = work.tile([P, C_OUT], F32, name="result")
-            nc.vector.scalar_tensor_tensor(
-                out=result[:],
-                in0=centred[(b, j)][:],
-                scalar=inv_stds[(b, j)][:],
-                in1=shift_all[:],
-                op0=ALU.mult,
-                op1=ALU.add,
-            )
+            nc.gpsimd.tensor_tensor(out=result[:], in0=gained[:], in1=shift_all[:], op=ALU.add)
             nc.sync.dma_start(
                 out=out[b].rearrange("(p j) c -> p j c", j=NODE_TILES)[:, j, :], in_=result[:]
             )
@@ -415,45 +411,45 @@ def tile_transformergraphconv_pa_t_kernel(
             if is_item(step - 3):
                 flip_weights(*item(step - 3))
 
-            done = divmod(turn - 2, NODE_TILES)
+            weighed = divmod(turn - 1, NODE_TILES)
+            done = divmod(turn - FINISH_LAG, NODE_TILES)
             if part == 0:
                 if batch_starting_at(turn + LOAD_LEAD) is not None:
                     load_batch(batch_starting_at(turn + LOAD_LEAD))
-                if is_head(turn - 1 + VALUES_LEAD):
-                    round_values(*divmod(turn - 1 + VALUES_LEAD, H))
-                if is_tile(turn - 2):
+                if is_tile(turn - FINISH_LAG):
                     invert_row_sums(*done)
                     add_conv_bias(*done)
-            if part == 1 and is_tile(turn - 2):
-                add_streams(*done)
-            if part == 2 and is_tile(turn - 2):
-                centre_and_gain(*done)
+            if part == 1:
+                if is_tile(turn - FINISH_LAG):
+                    add_streams(*done)
+                if is_head(turn + QK_LEAD):
+                    flip_queries_and_keys(*divmod(turn + QK_LEAD, H))
+            if part == 2:
+                if is_head(turn + QK_LEAD):
+                    keep_queries_and_keys(*divmod(turn + QK_LEAD, H))
+                if is_head(turn - 1 + VALUES_LEAD):
+                    round_values(*divmod(turn - 1 + VALUES_LEAD, H))
             if part == 3:
                 if batch_starting_at(turn - 1 + NODES_LEAD) is not None:
                     quantise_nodes(batch_starting_at(turn - 1 + NODES_LEAD))
                 if is_tile(turn - 1):
-                    quantise_weights(*divmod(turn - 1, NODE_TILES))
+                    quantise_weights(*weighed)
 
             if is_item(step - 1):
                 scale_row_maximum(*item(step - 1))
 
-            if part == 0 and is_tile(turn - 2):
+            if part == 0 and is_tile(turn - FINISH_LAG):
                 divide_by_row_sums(*done)
-            if part == 1:
-                if is_tile(turn - 2):
-                    negate_mean(*done)
-                    invert_deviation(*done)
+            if part == 1 and is_tile(turn - FINISH_LAG):
+                negate_mean(*done)
+                invert_deviation(*done)
+                normalise_and_store(*done)
+            if part == 3:
                 if is_head(turn - 1 + VALUES_LEAD):
                     quantise_values(*divmod(turn - 1 + VALUES_LEAD, H))
-            if part == 2:
-                if is_tile(turn - 3):
-                    normalise_and_store(*divmod(turn - 3, NODE_TILES))
-                if is_head(turn + QK_LEAD):
-                    flip_queries_and_keys(*divmod(turn + QK_LEAD, H))
-            if part == 3:
                 if is_tile(turn - 1):
-                    multiply_projection(*divmod(turn - 1, NODE_TILES))
-                    multiply_weights_and_values(*divmod(turn - 1, NODE_TILES))
+                    multiply_projection(*weighed)
+                    multiply_weights_and_values(*weighed)
                 if is_head(turn + VALUES_LEAD):
                     multiply_values(*divmod(turn + VALUES_LEAD, H))
                 if batch_starting_at(turn + NODES_LEAD) is not None:

@@ -31,7 +31,7 @@ TILES = B * NODE_TILES
 HEADS = B * H
 
 QK_LEAD = 4
-VALUES_LEAD = 3
+VALUES_LEAD = 2
 NODES_LEAD = 4
 LOAD_LEAD = 8
 FIRST_STEP = -H * LOAD_LEAD
@@ -416,6 +416,8 @@ def tile_transformergraphconv_pa_t_kernel(
             if part == 0:
                 if batch_starting_at(turn + LOAD_LEAD) is not None:
                     load_batch(batch_starting_at(turn + LOAD_LEAD))
+                if is_head(turn + VALUES_LEAD):
+                    multiply_values(*divmod(turn + VALUES_LEAD, H))
                 if is_tile(turn - FINISH_LAG):
                     invert_row_sums(*done)
                     add_conv_bias(*done)
@@ -425,10 +427,12 @@ def tile_transformergraphconv_pa_t_kernel(
                 if is_head(turn + QK_LEAD):
                     flip_queries_and_keys(*divmod(turn + QK_LEAD, H))
             if part == 2:
+                if is_tile(turn - 1):
+                    multiply_projection(*weighed)
                 if is_head(turn + QK_LEAD):
                     keep_queries_and_keys(*divmod(turn + QK_LEAD, H))
-                if is_head(turn - 1 + VALUES_LEAD):
-                    round_values(*divmod(turn - 1 + VALUES_LEAD, H))
+                if is_head(turn + VALUES_LEAD):
+                    round_values(*divmod(turn + VALUES_LEAD, H))
             if part == 3:
                 if batch_starting_at(turn - 1 + NODES_LEAD) is not None:
                     quantise_nodes(batch_starting_at(turn - 1 + NODES_LEAD))
@@ -445,12 +449,9 @@ def tile_transformergraphconv_pa_t_kernel(
                 invert_deviation(*done)
                 normalise_and_store(*done)
             if part == 3:
-                if is_head(turn - 1 + VALUES_LEAD):
-                    quantise_values(*divmod(turn - 1 + VALUES_LEAD, H))
-                if is_tile(turn - 1):
-                    multiply_projection(*weighed)
-                    multiply_weights_and_values(*weighed)
                 if is_head(turn + VALUES_LEAD):
-                    multiply_values(*divmod(turn + VALUES_LEAD, H))
+                    quantise_values(*divmod(turn + VALUES_LEAD, H))
+                if is_tile(turn - 1):
+                    multiply_weights_and_values(*weighed)
                 if batch_starting_at(turn + NODES_LEAD) is not None:
                     flip_nodes(batch_starting_at(turn + NODES_LEAD))

@@ -11,7 +11,6 @@ U8 = mybir.dt.uint8
 FP8X4 = mybir.dt.float8_e4m3fn_x4
 ALU = mybir.AluOpType
 ACT = mybir.ActivationFunctionType
-AXIS = mybir.AxisListType
 
 P = 128
 PACK = 4
@@ -30,13 +29,8 @@ ITEMS = B * NODE_TILES * H
 TILES = B * NODE_TILES
 HEADS = B * H
 
-QK_LEAD = 4
-VALUES_LEAD = 2
-NODES_LEAD = 4
-LOAD_LEAD = 8
-FIRST_STEP = -H * LOAD_LEAD
-FINISH_LAG = 2
-LAST_STEP = H * (TILES - 1 + FINISH_LAG) + 2
+FIRST_ROUND = -8
+LAST_STEP = H * (TILES - 1 + 5) + 2
 
 
 def tile_transformergraphconv_pa_t_kernel(
@@ -49,9 +43,9 @@ def tile_transformergraphconv_pa_t_kernel(
         rows_pool = ctx.enter_context(tc.tile_pool(name="rows", bufs=2))
         batch_pool = ctx.enter_context(tc.tile_pool(name="batch", bufs=3))
         work = ctx.enter_context(tc.tile_pool(name="work", bufs=3))
-        small = ctx.enter_context(tc.tile_pool(name="small", bufs=4))
-        score_banks = ctx.enter_context(tc.psum_pool(name="score_banks", bufs=3))
-        flip_banks = ctx.enter_context(tc.psum_pool(name="flip_banks", bufs=2))
+        small = ctx.enter_context(tc.tile_pool(name="small", bufs=8))
+        score_banks = ctx.enter_context(tc.psum_pool(name="score_banks", bufs=2))
+        flip_banks = ctx.enter_context(tc.psum_pool(name="flip_banks", bufs=3))
         product_banks = ctx.enter_context(tc.psum_pool(name="product_banks", bufs=3))
 
         def head_cols(h):
@@ -68,36 +62,39 @@ def tile_transformergraphconv_pa_t_kernel(
                 out=q_tile[:].rearrange("p h j d -> p h (j d)"),
                 in_=q[b].rearrange("h (p j) d -> p h (j d)", j=NODE_TILES),
             )
-            k_tile = rows_pool.tile([P, H, NODE_TILES, DH], BF16, name="k_tile")
-            nc.sync.dma_start(
-                out=k_tile[:].rearrange("p h j d -> p h (j d)"),
-                in_=k[b].rearrange("h (p j) d -> p h (j d)", j=NODE_TILES),
-            )
+            k_tile = rows_pool.tile([P, H, 2, 2, DH], BF16, name="k_tile")
+            for a in range(2):
+                nc.sync.dma_start(
+                    out=k_tile[:, :, a, :, :].rearrange("p h u d -> p h (u d)"),
+                    in_=k[b][:, a * 2 * P : (a + 1) * 2 * P, :].rearrange(
+                        "h (p u) d -> p h (u d)", u=2
+                    ),
+                )
             x_tile = rows_pool.tile([P, NODE_TILES * C_IN], BF16, name="x_tile")
             nc.sync.dma_start(
                 out=x_tile[:], in_=x[b].rearrange("(p j) c -> p (j c)", j=NODE_TILES)
             )
             q_rows[b], k_rows[b], x_rows[b] = q_tile, k_tile, x_tile
 
-        def flip_channels(rows):
+        def transpose_channels(rows, pair):
             words = rows.bitcast(F32)
-            grouped = work.tile([P, PACK * P * PACK], BF16, name="grouped", align_bytes=64)
+            flipped = flip_banks.tile([P, 2, 2 * P], F32, name="flipped", tag="flip")
+            for i in range(2):
+                for u in range(2):
+                    first_word = (2 * pair + i) * (C_IN // 2) + u * P
+                    nc.tensor.transpose(
+                        flipped[:, u, tile_cols(i)],
+                        words[:, first_word : first_word + P],
+                        ident_f32[:],
+                    )
+            return flipped
+
+        def keep_channels(flipped, grouped, pair):
             grouped_words = grouped[:].bitcast(F32).rearrange("p (c u) -> p c u", u=2)
-            for pair in range(2):
-                flipped = flip_banks.tile([P, 2, 2 * P], F32, name="flipped", tag="flip")
-                for i in range(2):
-                    for u in range(2):
-                        first_word = (2 * pair + i) * (C_IN // 2) + u * P
-                        nc.tensor.transpose(
-                            flipped[:, u, tile_cols(i)],
-                            words[:, first_word : first_word + P],
-                            ident_f32[:],
-                        )
-                nc.scalar.copy(
-                    out=grouped_words[:, pair * 2 * P : (pair + 1) * 2 * P, :],
-                    in_=flipped[:].rearrange("p u c -> p c u"),
-                )
-            return grouped
+            nc.scalar.copy(
+                out=grouped_words[:, pair * 2 * P : (pair + 1) * 2 * P, :],
+                in_=flipped[:].rearrange("p u c -> p c u"),
+            )
 
         cw_rows = const.tile([P, PACK * C_IN], BF16, name="cw_rows")
         nc.scalar.dma_start(
@@ -126,26 +123,38 @@ def tile_transformergraphconv_pa_t_kernel(
         minus_half = const.tile([P, 1], F32, name="minus_half")
         nc.vector.memset(minus_half[:], -0.5)
 
-        cw_grouped = flip_channels(cw_rows[:])
+        def prepare_weights():
+            cw_grouped = work.tile([P, PACK * P * PACK], BF16, name="grouped", align_bytes=64, bufs=2)
+            for pair in range(2):
+                keep_channels(transpose_channels(cw_rows[:], pair), cw_grouped, pair)
+            nc.vector.quantize_mx(
+                out=cw_codes[:].bitcast(FP8X4), scales=cw_scales[:], in_=cw_grouped[:]
+            )
+            wv_grouped = const.tile([P, H, DH, PACK], BF16, name="wv_grouped", align_bytes=64)
+            nc.vector.tensor_copy(out=wv_grouped[:], in_=wv_rows[:].rearrange("p h t d -> p h d t"))
+            nc.vector.quantize_mx(
+                out=wv_codes[:].bitcast(FP8X4),
+                scales=wv_scales[:],
+                in_=wv_grouped[:].rearrange("p h d t -> p (h d t)"),
+            )
+
         cw_codes = const.tile([P, C_OUT], U32, name="cw_codes", align_bytes=64)
         cw_scales = const.tile([P, C_OUT], U8, name="cw_scales", align_bytes=64)
-        nc.vector.quantize_mx(
-            out=cw_codes[:].bitcast(FP8X4), scales=cw_scales[:], in_=cw_grouped[:]
-        )
-        wv_grouped = const.tile([P, H, DH, PACK], BF16, name="wv_grouped", align_bytes=64)
-        nc.vector.tensor_copy(out=wv_grouped[:], in_=wv_rows[:].rearrange("p h t d -> p h d t"))
         wv_codes = const.tile([P, H * DH], U32, name="wv_codes", align_bytes=64)
         wv_scales = const.tile([P, H * DH], U8, name="wv_scales", align_bytes=64)
-        nc.vector.quantize_mx(
-            out=wv_codes[:].bitcast(FP8X4),
-            scales=wv_scales[:],
-            in_=wv_grouped[:].rearrange("p h d t -> p (h d t)"),
-        )
 
-        x_grouped, x_codes, x_scales = {}, {}, {}
+        x_banks, x_grouped, x_codes, x_scales = {}, {}, {}, {}
 
-        def flip_nodes(b):
-            x_grouped[b] = flip_channels(x_rows[b][:])
+        def flip_nodes(b, pair):
+            x_banks[(b, pair)] = transpose_channels(x_rows[b][:], pair)
+
+        def keep_nodes(b, pair):
+            if pair == 0:
+                grouped = work.tile(
+                    [P, PACK * P * PACK], BF16, name="grouped", align_bytes=64, bufs=2
+                )
+                x_grouped[b] = grouped
+            keep_channels(x_banks[(b, pair)], x_grouped[b], pair)
 
         def quantise_nodes(b):
             xc = batch_pool.tile([P, N], U32, name="xc", align_bytes=64)
@@ -160,21 +169,26 @@ def tile_transformergraphconv_pa_t_kernel(
             flipped = flip_banks.tile([P, 2, N], BF16, name="flipped", tag="flip")
             for j in range(NODE_TILES):
                 nc.tensor.transpose(flipped[:, 0, tile_cols(j)], q_rows[b][:, h, j, :], ident_bf16[:])
-                nc.tensor.transpose(flipped[:, 1, tile_cols(j)], k_rows[b][:, h, j, :], ident_bf16[:])
+            for u in range(2):
+                for a in range(2):
+                    nc.tensor.transpose(
+                        flipped[:, 1, tile_cols(2 * u + a)], k_rows[b][:, h, a, u, :], ident_bf16[:]
+                    )
             qk_banks[(b, h)] = flipped
 
         def keep_queries_and_keys(b, h):
             qk = batch_pool.tile([P, 2, N], BF16, name="qk", bufs=3 * H)
-            nc.vector.tensor_copy(out=qk[:], in_=qk_banks[(b, h)][:])
+            nc.scalar.copy(out=qk[:], in_=qk_banks[(b, h)][:])
             qk_flipped[(b, h)] = qk
 
         def multiply_values(b, h):
             values = product_banks.tile([P, PACK, DH], F32, name="values", tag="product")
             for t in range(PACK):
+                j = 2 * (t % 2) + t // 2
                 nc.tensor.matmul_mx(
                     out=values[:, t, :],
-                    lhsT=x_codes[b][:, tile_cols(t)].bitcast(FP8X4),
-                    lhsT_scale=x_scales[b][:, tile_cols(t)],
+                    lhsT=x_codes[b][:, tile_cols(j)].bitcast(FP8X4),
+                    lhsT_scale=x_scales[b][:, tile_cols(j)],
                     rhs=wv_codes[:, head_cols(h)].bitcast(FP8X4),
                     rhs_scale=wv_scales[:, head_cols(h)],
                     start=True,
@@ -197,8 +211,8 @@ def tile_transformergraphconv_pa_t_kernel(
             )
             v_codes[(b, h)], v_scales[(b, h)] = vc, vs
 
-        scores, row_max, exp_bias, e_rows = {}, {}, {}, {}
-        row_sums, e_grouped = {}, {}
+        scores, neg_scores, exp_bias, e_rows = {}, {}, {}, {}
+        row_sums, e_banks, e_grouped = {}, {}, {}
 
         def multiply_scores(b, j, h):
             s = score_banks.tile([P, N], F32, name="s", tag="scores")
@@ -211,57 +225,62 @@ def tile_transformergraphconv_pa_t_kernel(
             )
             scores[(b, j, h)] = s
 
-        def find_row_maximum(b, j, h):
-            top = small.tile([P, 1], F32, name="top")
-            nc.vector.tensor_reduce(out=top[:], in_=scores[(b, j, h)][:], axis=AXIS.X, op=ALU.max)
-            row_max[(b, j, h)] = top
-
-        def scale_row_maximum(b, j, h):
-            shift = small.tile([P, 1], F32, name="shift")
+        def scale_and_find_maximum(b, j, h):
+            ns = work.tile([P, N], F32, name="ns", bufs=6)
+            nb = small.tile([P, 1], F32, name="nb")
             nc.vector.tensor_scalar(
-                out=shift[:],
-                in0=row_max[(b, j, h)][:],
+                out=ns[:],
+                in0=scores[(b, j, h)][:],
                 scalar1=-SCORE_SCALE,
                 scalar2=None,
                 op0=ALU.mult,
+                op1=ALU.min,
+                accum_out=nb[:],
             )
-            exp_bias[(b, j, h)] = shift
+            neg_scores[(b, j, h)], exp_bias[(b, j, h)] = ns, nb
 
         def exponentiate(b, j, h):
             if h == 0:
                 row_sum = small.tile([P, H], F32, name="row_sum")
                 row_sums[(b, j)] = row_sum
-            e_item = work.tile([P, N], BF16, name="e_item")
+            e_item = work.tile([P, N], BF16, name="e_item", bufs=6)
             nc.scalar.activation(
                 out=e_item[:],
-                in_=scores[(b, j, h)][:],
+                in_=neg_scores[(b, j, h)][:],
                 func=ACT.Exp,
                 bias=exp_bias[(b, j, h)][:],
-                scale=SCORE_SCALE,
+                scale=-1.0,
                 accum_out=row_sums[(b, j)][:, h : h + 1],
             )
             e_rows[(b, j, h)] = e_item
 
-        def flip_weights(b, j, h):
-            if h == 0:
-                eg = work.tile([P, H, P, PACK], BF16, name="eg", align_bytes=64)
+        def flip_weights(b, j, first):
+            flipped = flip_banks.tile([P, 2, 2, P], F32, name="flipped", tag="flip")
+            for i in range(2):
+                words = e_rows[(b, j, first + i)][:].bitcast(F32)
+                for u in range(2):
+                    nc.tensor.transpose(flipped[:, i, u, :], words[:, tile_cols(u)], ident_f32[:])
+            e_banks[(b, j, first)] = flipped
+
+        def keep_weights(b, j, first):
+            if first == 0:
+                eg = work.tile([P, H * P * PACK], BF16, name="eg", align_bytes=64)
                 e_grouped[(b, j)] = eg
-            flipped = flip_banks.tile([P, PACK, P], BF16, name="flipped", tag="flip")
-            for t in range(PACK):
-                nc.tensor.transpose(flipped[:, t, :], e_rows[(b, j, h)][:, tile_cols(t)], ident_bf16[:])
-            nc.scalar.copy(out=e_grouped[(b, j)][:, h], in_=flipped[:].rearrange("p t n -> p n t"))
+            eg_words = e_grouped[(b, j)][:].bitcast(F32).rearrange("p (h n u) -> p h n u", h=H, u=2)
+            nc.scalar.copy(
+                out=eg_words[:, first : first + 2, :, :],
+                in_=e_banks[(b, j, first)][:].rearrange("p i u n -> p i n u"),
+            )
 
         e_codes, e_scales, attended, projected = {}, {}, {}, {}
-        inv_sums, conv, mixed, y_tiles, neg_means, inv_stds = {}, {}, {}, {}, {}, {}
+        inv_sums, conv, mixed, y_tiles, y_sums, neg_means, inv_stds, centred = (
+            {}, {}, {}, {}, {}, {}, {}, {},
+        )
 
         def quantise_weights(b, j):
             ec = work.tile([P, H * P], U32, name="ec", align_bytes=64)
             es = work.tile([P, H * P], U8, name="es", align_bytes=64)
-            nc.vector.quantize_mx(
-                out=ec[:].bitcast(FP8X4),
-                scales=es[:],
-                in_=e_grouped[(b, j)][:].rearrange("p h n t -> p (h n t)"),
-            )
+            nc.vector.quantize_mx(out=ec[:].bitcast(FP8X4), scales=es[:], in_=e_grouped[(b, j)][:])
             e_codes[(b, j)], e_scales[(b, j)] = ec, es
 
         def multiply_projection(b, j):
@@ -297,7 +316,7 @@ def tile_transformergraphconv_pa_t_kernel(
             inv_sums[(b, j)] = inv_sum
 
         def add_conv_bias(b, j):
-            cv = work.tile([P, C_OUT], F32, name="cv")
+            cv = work.tile([P, C_OUT], F32, name="cv", bufs=6)
             nc.vector.tensor_tensor(out=cv[:], in0=projected[(b, j)][:], in1=bias_all[:], op=ALU.add)
             conv[(b, j)] = cv
 
@@ -310,8 +329,6 @@ def tile_transformergraphconv_pa_t_kernel(
                 op=ALU.mult,
             )
             mixed[(b, j)] = scaled
-
-        y_sums = {}
 
         def add_streams(b, j):
             y = work.tile([P, C_OUT], F32, name="y")
@@ -339,7 +356,7 @@ def tile_transformergraphconv_pa_t_kernel(
             neg_means[(b, j)] = neg_mean
 
         def invert_deviation(b, j):
-            squares = work.tile([P, C_OUT], BF16, name="squares")
+            squares = work.tile([P, C_OUT], BF16, name="squares", bufs=2)
             square_sum = small.tile([P, 1], F32, name="square_sum")
             nc.scalar.activation(
                 out=squares[:],
@@ -362,20 +379,28 @@ def tile_transformergraphconv_pa_t_kernel(
             nc.gpsimd.tensor_tensor(out=inv_std[:], in0=var_eps[:], in1=minus_half[:], op=ALU.pow)
             inv_stds[(b, j)] = inv_std
 
-        def normalise_and_store(b, j):
-            z = work.tile([P, C_OUT], F32, name="z")
-            nc.gpsimd.tensor_scalar(
-                out=z[:],
+        def centre_and_gain(b, j):
+            t = work.tile([P, C_OUT], F32, name="t")
+            nc.vector.scalar_tensor_tensor(
+                out=t[:],
                 in0=y_tiles[(b, j)][:],
-                scalar1=neg_means[(b, j)][:],
-                scalar2=inv_stds[(b, j)][:],
+                scalar=neg_means[(b, j)][:],
+                in1=gain_all[:],
                 op0=ALU.add,
                 op1=ALU.mult,
             )
-            gained = work.tile([P, C_OUT], F32, name="gained")
-            nc.gpsimd.tensor_tensor(out=gained[:], in0=z[:], in1=gain_all[:], op=ALU.mult)
-            result = work.tile([P, C_OUT], F32, name="result")
-            nc.gpsimd.tensor_tensor(out=result[:], in0=gained[:], in1=shift_all[:], op=ALU.add)
+            centred[(b, j)] = t
+
+        def normalise_and_store(b, j):
+            result = work.tile([P, C_OUT], F32, name="result", bufs=4)
+            nc.vector.scalar_tensor_tensor(
+                out=result[:],
+                in0=centred[(b, j)][:],
+                scalar=inv_stds[(b, j)][:],
+                in1=shift_all[:],
+                op0=ALU.mult,
+                op1=ALU.add,
+            )
             nc.sync.dma_start(
                 out=out[b].rearrange("(p j) c -> p j c", j=NODE_TILES)[:, j, :], in_=result[:]
             )
@@ -394,64 +419,88 @@ def tile_transformergraphconv_pa_t_kernel(
         def is_head(m):
             return 0 <= m < HEADS
 
+        def tile_of(n):
+            return divmod(n, NODE_TILES)
+
+        def head_of(m):
+            return divmod(m, H)
+
         def batch_starting_at(n):
             if is_tile(n) and n % NODE_TILES == 0:
                 return n // NODE_TILES
             return None
 
-        for step in range(FIRST_STEP, LAST_STEP):
+        for step in range(H * FIRST_ROUND, LAST_STEP):
             turn, part = divmod(step, H)
 
+            if part == 0 and batch_starting_at(turn + 8) is not None:
+                load_batch(batch_starting_at(turn + 8))
+            if step == -5 * H:
+                prepare_weights()
+
+            if part == 1 and is_tile(turn):
+                multiply_projection(*tile_of(turn))
             if is_item(step):
                 multiply_scores(*item(step))
+            if part == 0 and is_tile(turn - 3):
+                multiply_weights_and_values(*tile_of(turn - 3))
+            if part == 1 and is_tile(turn - 1):
+                flip_weights(*tile_of(turn - 1), 0)
+            if part == 2:
+                if is_head(turn + 4):
+                    flip_queries_and_keys(*head_of(turn + 4))
+                if batch_starting_at(turn + 7) is not None:
+                    flip_nodes(batch_starting_at(turn + 7), 0)
+                if batch_starting_at(turn + 6) is not None:
+                    flip_nodes(batch_starting_at(turn + 6), 1)
+            if part == 3:
+                if is_tile(turn - 1):
+                    flip_weights(*tile_of(turn - 1), 2)
+                if is_head(turn + 3):
+                    multiply_values(*head_of(turn + 3))
+
             if is_item(step - 1):
-                find_row_maximum(*item(step - 1))
+                scale_and_find_maximum(*item(step - 1))
+            if part == 0:
+                if is_tile(turn - 4):
+                    add_streams(*tile_of(turn - 4))
+                if is_head(turn + 1):
+                    quantise_values(*head_of(turn + 1))
+            if part == 1:
+                if is_tile(turn - 4):
+                    negate_mean(*tile_of(turn - 4))
+                if is_tile(turn - 2):
+                    invert_row_sums(*tile_of(turn - 2))
+                if is_tile(turn - 3):
+                    divide_by_row_sums(*tile_of(turn - 3))
+                if is_tile(turn - 5):
+                    normalise_and_store(*tile_of(turn - 5))
+            if part == 2:
+                if is_tile(turn - 2):
+                    quantise_weights(*tile_of(turn - 2))
+                if is_tile(turn - 4):
+                    centre_and_gain(*tile_of(turn - 4))
+            if part == 3:
+                if is_tile(turn):
+                    add_conv_bias(*tile_of(turn))
+                if batch_starting_at(turn + 4) is not None:
+                    quantise_nodes(batch_starting_at(turn + 4))
+
             if is_item(step - 2):
                 exponentiate(*item(step - 2))
-            if is_item(step - 3):
-                flip_weights(*item(step - 3))
-
-            weighed = divmod(turn - 1, NODE_TILES)
-            done = divmod(turn - FINISH_LAG, NODE_TILES)
             if part == 0:
-                if batch_starting_at(turn + LOAD_LEAD) is not None:
-                    load_batch(batch_starting_at(turn + LOAD_LEAD))
-                if is_head(turn + VALUES_LEAD):
-                    multiply_values(*divmod(turn + VALUES_LEAD, H))
-                if is_tile(turn - FINISH_LAG):
-                    invert_row_sums(*done)
-                    add_conv_bias(*done)
-            if part == 1:
-                if is_tile(turn - FINISH_LAG):
-                    add_streams(*done)
-                if is_head(turn + QK_LEAD):
-                    flip_queries_and_keys(*divmod(turn + QK_LEAD, H))
-            if part == 2:
-                if is_tile(turn - 1):
-                    multiply_projection(*weighed)
-                if is_head(turn + QK_LEAD):
-                    keep_queries_and_keys(*divmod(turn + QK_LEAD, H))
-                if is_head(turn + VALUES_LEAD):
-                    round_values(*divmod(turn + VALUES_LEAD, H))
+                if is_tile(turn - 2):
+                    keep_weights(*tile_of(turn - 2), 2)
+                if batch_starting_at(turn + 6) is not None:
+                    keep_nodes(batch_starting_at(turn + 6), 0)
+                if batch_starting_at(turn + 5) is not None:
+                    keep_nodes(batch_starting_at(turn + 5), 1)
+            if part == 1 and is_head(turn + 2):
+                round_values(*head_of(turn + 2))
+            if part == 2 and is_tile(turn - 1):
+                keep_weights(*tile_of(turn - 1), 0)
             if part == 3:
-                if batch_starting_at(turn - 1 + NODES_LEAD) is not None:
-                    quantise_nodes(batch_starting_at(turn - 1 + NODES_LEAD))
-                if is_tile(turn - 1):
-                    quantise_weights(*weighed)
-
-            if is_item(step - 1):
-                scale_row_maximum(*item(step - 1))
-
-            if part == 0 and is_tile(turn - FINISH_LAG):
-                divide_by_row_sums(*done)
-            if part == 1 and is_tile(turn - FINISH_LAG):
-                negate_mean(*done)
-                invert_deviation(*done)
-                normalise_and_store(*done)
-            if part == 3:
-                if is_head(turn + VALUES_LEAD):
-                    quantise_values(*divmod(turn + VALUES_LEAD, H))
-                if is_tile(turn - 1):
-                    multiply_weights_and_values(*weighed)
-                if batch_starting_at(turn + NODES_LEAD) is not None:
-                    flip_nodes(batch_starting_at(turn + NODES_LEAD))
+                if is_head(turn + 4):
+                    keep_queries_and_keys(*head_of(turn + 4))
+                if is_tile(turn - 4):
+                    invert_deviation(*tile_of(turn - 4))

@@ -122,6 +122,8 @@ def tile_transformergraphconv_pa_t_kernel(
         make_identity(nc, ident_bf16[:])
         minus_half = const.tile([P, 1], F32, name="minus_half")
         nc.vector.memset(minus_half[:], -0.5)
+        minus_one = const.tile([P, H], F32, name="minus_one")
+        nc.vector.memset(minus_one[:], -1.0)
 
         def prepare_weights():
             cw_grouped = work.tile([P, PACK * P * PACK], BF16, name="grouped", align_bytes=64, bufs=2)
@@ -312,7 +314,9 @@ def tile_transformergraphconv_pa_t_kernel(
 
         def invert_row_sums(b, j):
             inv_sum = small.tile([P, H], F32, name="inv_sum")
-            nc.vector.reciprocal(inv_sum[:], row_sums[(b, j)][:])
+            nc.gpsimd.tensor_tensor(
+                out=inv_sum[:], in0=row_sums[(b, j)][:], in1=minus_one[:], op=ALU.pow
+            )
             inv_sums[(b, j)] = inv_sum
 
         def add_conv_bias(b, j):
@@ -322,12 +326,13 @@ def tile_transformergraphconv_pa_t_kernel(
 
         def divide_by_row_sums(b, j):
             scaled = work.tile([P, H, DH], F32, name="scaled")
-            nc.vector.tensor_tensor(
-                out=scaled[:],
-                in0=attended[(b, j)][:],
-                in1=inv_sums[(b, j)][:].unsqueeze(2).to_broadcast([P, H, DH]),
-                op=ALU.mult,
-            )
+            for h in range(H):
+                nc.scalar.activation(
+                    out=scaled[:, h, :],
+                    in_=attended[(b, j)][:, h, :],
+                    func=ACT.Relu,
+                    scale=inv_sums[(b, j)][:, h : h + 1],
+                )
             mixed[(b, j)] = scaled
 
         def add_streams(b, j):
@@ -346,12 +351,13 @@ def tile_transformergraphconv_pa_t_kernel(
 
         def negate_mean(b, j):
             neg_mean = small.tile([P, 1], F32, name="neg_mean")
-            nc.vector.tensor_scalar(
+            nc.gpsimd.tensor_scalar(
                 out=neg_mean[:],
                 in0=y_sums[(b, j)][:],
                 scalar1=-1.0 / C_OUT,
-                scalar2=None,
+                scalar2=0.0,
                 op0=ALU.mult,
+                op1=ALU.add,
             )
             neg_means[(b, j)] = neg_mean
 
@@ -461,46 +467,43 @@ def tile_transformergraphconv_pa_t_kernel(
 
             if is_item(step - 1):
                 scale_and_find_maximum(*item(step - 1))
-            if part == 0:
-                if is_tile(turn - 4):
-                    add_streams(*tile_of(turn - 4))
-                if is_head(turn + 1):
-                    quantise_values(*head_of(turn + 1))
-            if part == 1:
-                if is_tile(turn - 4):
-                    negate_mean(*tile_of(turn - 4))
-                if is_tile(turn - 2):
-                    invert_row_sums(*tile_of(turn - 2))
-                if is_tile(turn - 3):
-                    divide_by_row_sums(*tile_of(turn - 3))
-                if is_tile(turn - 5):
-                    normalise_and_store(*tile_of(turn - 5))
+            if part == 0 and is_tile(turn - 4):
+                add_streams(*tile_of(turn - 4))
+                negate_mean(*tile_of(turn - 4))
+            if part == 1 and is_tile(turn - 5):
+                normalise_and_store(*tile_of(turn - 5))
             if part == 2:
                 if is_tile(turn - 2):
                     quantise_weights(*tile_of(turn - 2))
-                if is_tile(turn - 4):
-                    centre_and_gain(*tile_of(turn - 4))
+                if is_head(turn + 1):
+                    quantise_values(*head_of(turn + 1))
+                if batch_starting_at(turn + 4) is not None:
+                    quantise_nodes(batch_starting_at(turn + 4))
             if part == 3:
                 if is_tile(turn):
                     add_conv_bias(*tile_of(turn))
-                if batch_starting_at(turn + 4) is not None:
-                    quantise_nodes(batch_starting_at(turn + 4))
+                if is_tile(turn - 4):
+                    centre_and_gain(*tile_of(turn - 4))
 
             if is_item(step - 2):
                 exponentiate(*item(step - 2))
             if part == 0:
                 if is_tile(turn - 2):
                     keep_weights(*tile_of(turn - 2), 2)
+                    invert_row_sums(*tile_of(turn - 2))
                 if batch_starting_at(turn + 6) is not None:
                     keep_nodes(batch_starting_at(turn + 6), 0)
                 if batch_starting_at(turn + 5) is not None:
                     keep_nodes(batch_starting_at(turn + 5), 1)
-            if part == 1 and is_head(turn + 2):
-                round_values(*head_of(turn + 2))
-            if part == 2 and is_tile(turn - 1):
-                keep_weights(*tile_of(turn - 1), 0)
-            if part == 3:
-                if is_head(turn + 4):
-                    keep_queries_and_keys(*head_of(turn + 4))
+            if part == 1:
+                if is_head(turn + 2):
+                    round_values(*head_of(turn + 2))
+                if is_tile(turn - 3):
+                    divide_by_row_sums(*tile_of(turn - 3))
+            if part == 2:
+                if is_tile(turn - 1):
+                    keep_weights(*tile_of(turn - 1), 0)
                 if is_tile(turn - 4):
                     invert_deviation(*tile_of(turn - 4))
+            if part == 3 and is_head(turn + 4):
+                keep_queries_and_keys(*head_of(turn + 4))

@@ -29,9 +29,6 @@ ITEMS = B * NODE_TILES * H
 TILES = B * NODE_TILES
 HEADS = B * H
 
-FIRST_ROUND = -8
-LAST_STEP = H * (TILES - 1 + 5) + 2
-
 
 def tile_transformergraphconv_pa_t_kernel(
     tc, x, q, k, W_v, conv_w, conv_b, ln_w, ln_b, out
@@ -56,25 +53,26 @@ def tile_transformergraphconv_pa_t_kernel(
 
         x_rows, q_rows, k_rows = {}, {}, {}
 
-        def load_batch(b):
-            q_tile = rows_pool.tile([P, H, NODE_TILES, DH], BF16, name="q_tile")
+        def load_queries_and_keys(b, h):
+            if h == 0:
+                q_tile = rows_pool.tile([P, H, NODE_TILES, DH], BF16, name="q_tile")
+                k_tile = rows_pool.tile([P, H, 2, 2, DH], BF16, name="k_tile")
+                q_rows[b], k_rows[b] = q_tile, k_tile
             nc.sync.dma_start(
-                out=q_tile[:].rearrange("p h j d -> p h (j d)"),
-                in_=q[b].rearrange("h (p j) d -> p h (j d)", j=NODE_TILES),
+                out=q_rows[b][:, h, :, :].rearrange("p j d -> p (j d)"),
+                in_=q[b][h].rearrange("(p j) d -> p (j d)", j=NODE_TILES),
             )
-            k_tile = rows_pool.tile([P, H, 2, 2, DH], BF16, name="k_tile")
-            for a in range(2):
-                nc.sync.dma_start(
-                    out=k_tile[:, :, a, :, :].rearrange("p h u d -> p h (u d)"),
-                    in_=k[b][:, a * 2 * P : (a + 1) * 2 * P, :].rearrange(
-                        "h (p u) d -> p h (u d)", u=2
-                    ),
-                )
+            nc.sync.dma_start(
+                out=k_rows[b][:, h, :, :, :].rearrange("p a u d -> p a (u d)"),
+                in_=k[b][h].rearrange("(a p u) d -> p a (u d)", a=2, u=2),
+            )
+
+        def load_nodes(b):
             x_tile = rows_pool.tile([P, NODE_TILES * C_IN], BF16, name="x_tile")
             nc.sync.dma_start(
                 out=x_tile[:], in_=x[b].rearrange("(p j) c -> p (j c)", j=NODE_TILES)
             )
-            q_rows[b], k_rows[b], x_rows[b] = q_tile, k_tile, x_tile
+            x_rows[b] = x_tile
 
         def transpose_channels(rows, pair):
             words = rows.bitcast(F32)
@@ -97,24 +95,30 @@ def tile_transformergraphconv_pa_t_kernel(
             )
 
         cw_rows = const.tile([P, PACK * C_IN], BF16, name="cw_rows")
-        nc.scalar.dma_start(
-            out=cw_rows[:].rearrange("p (r c) -> p r c", c=C_IN),
-            in_=conv_w.rearrange("(r p) c -> p r c", p=P),
-        )
         wv_rows = const.tile([P, H, PACK, DH], BF16, name="wv_rows")
-        for u in range(2):
-            nc.scalar.dma_start(
-                out=wv_rows[:, :, 2 * u : 2 * u + 2, :].rearrange("p h i d -> p h (i d)"),
-                in_=W_v[:, u * 2 * P : (u + 1) * 2 * P, :].rearrange(
-                    "h (p i) d -> p h (i d)", i=2
-                ),
-            )
         bias_all = const.tile([P, C_OUT], BF16, name="bias_all")
-        nc.scalar.dma_start(out=bias_all[:], in_=conv_b.partition_broadcast(P))
         gain_all = const.tile([P, C_OUT], BF16, name="gain_all")
-        nc.scalar.dma_start(out=gain_all[:], in_=ln_w.partition_broadcast(P))
         shift_all = const.tile([P, C_OUT], BF16, name="shift_all")
-        nc.scalar.dma_start(out=shift_all[:], in_=ln_b.partition_broadcast(P))
+
+        def load_value_weights():
+            for u in range(2):
+                nc.sync.dma_start(
+                    out=wv_rows[:, :, 2 * u : 2 * u + 2, :].rearrange("p h i d -> p h (i d)"),
+                    in_=W_v[:, u * 2 * P : (u + 1) * 2 * P, :].rearrange(
+                        "h (p i) d -> p h (i d)", i=2
+                    ),
+                )
+
+        def load_conv_weights():
+            nc.sync.dma_start(
+                out=cw_rows[:].rearrange("p (r c) -> p r c", c=C_IN),
+                in_=conv_w.rearrange("(r p) c -> p r c", p=P),
+            )
+
+        def load_channel_vectors():
+            nc.sync.dma_start(out=bias_all[:], in_=conv_b.partition_broadcast(P))
+            nc.sync.dma_start(out=gain_all[:], in_=ln_w.partition_broadcast(P))
+            nc.sync.dma_start(out=shift_all[:], in_=ln_b.partition_broadcast(P))
 
         ident_f32 = const.tile([P, P], F32, name="ident_f32")
         make_identity(nc, ident_f32[:])
@@ -125,21 +129,35 @@ def tile_transformergraphconv_pa_t_kernel(
         minus_one = const.tile([P, H], F32, name="minus_one")
         nc.vector.memset(minus_one[:], -1.0)
 
-        def prepare_weights():
-            cw_grouped = work.tile([P, PACK * P * PACK], BF16, name="grouped", align_bytes=64, bufs=2)
-            for pair in range(2):
-                keep_channels(transpose_channels(cw_rows[:], pair), cw_grouped, pair)
+        cw_banks, cw_grouped = {}, {}
+
+        def flip_conv_weights(pair):
+            cw_banks[pair] = transpose_channels(cw_rows[:], pair)
+
+        def keep_conv_weights(pair):
+            if pair == 0:
+                grouped = work.tile(
+                    [P, PACK * P * PACK], BF16, name="grouped", align_bytes=64, bufs=2
+                )
+                cw_grouped[0] = grouped
+            keep_channels(cw_banks[pair], cw_grouped[0], pair)
+
+        def quantise_conv_weights():
             nc.vector.quantize_mx(
-                out=cw_codes[:].bitcast(FP8X4), scales=cw_scales[:], in_=cw_grouped[:]
+                out=cw_codes[:].bitcast(FP8X4), scales=cw_scales[:], in_=cw_grouped[0][:]
             )
-            wv_grouped = const.tile([P, H, DH, PACK], BF16, name="wv_grouped", align_bytes=64)
+
+        def group_value_weights():
             nc.vector.tensor_copy(out=wv_grouped[:], in_=wv_rows[:].rearrange("p h t d -> p h d t"))
+
+        def quantise_value_weights():
             nc.vector.quantize_mx(
                 out=wv_codes[:].bitcast(FP8X4),
                 scales=wv_scales[:],
                 in_=wv_grouped[:].rearrange("p h d t -> p (h d t)"),
             )
 
+        wv_grouped = const.tile([P, H, DH, PACK], BF16, name="wv_grouped", align_bytes=64)
         cw_codes = const.tile([P, C_OUT], U32, name="cw_codes", align_bytes=64)
         cw_scales = const.tile([P, C_OUT], U8, name="cw_scales", align_bytes=64)
         wv_codes = const.tile([P, H * DH], U32, name="wv_codes", align_bytes=64)
@@ -199,7 +217,7 @@ def tile_transformergraphconv_pa_t_kernel(
             value_banks[(b, h)] = values
 
         def round_values(b, h):
-            vg = work.tile([P, DH, PACK], BF16, name="vg", align_bytes=64)
+            vg = work.tile([P, DH, PACK], BF16, name="vg", align_bytes=64, bufs=4)
             nc.scalar.copy(out=vg[:], in_=value_banks[(b, h)][:].rearrange("p t d -> p d t"))
             v_grouped[(b, h)] = vg
 
@@ -416,94 +434,100 @@ def tile_transformergraphconv_pa_t_kernel(
             j, h = divmod(rest, H)
             return b, j, h
 
-        def is_item(i):
-            return 0 <= i < ITEMS
-
-        def is_tile(n):
-            return 0 <= n < TILES
-
-        def is_head(m):
-            return 0 <= m < HEADS
-
         def tile_of(n):
             return divmod(n, NODE_TILES)
 
         def head_of(m):
             return divmod(m, H)
 
-        def batch_starting_at(n):
-            if is_tile(n) and n % NODE_TILES == 0:
-                return n // NODE_TILES
-            return None
+        plan = {}
 
-        for step in range(H * FIRST_ROUND, LAST_STEP):
-            turn, part = divmod(step, H)
+        def put(step, place, work_of, *args):
+            plan.setdefault(step, []).append((place, work_of, args))
 
-            if part == 0 and batch_starting_at(turn + 8) is not None:
-                load_batch(batch_starting_at(turn + 8))
-            if step == -5 * H:
-                prepare_weights()
+        def at(turn, part):
+            return H * turn + part
 
-            if part == 1 and is_tile(turn):
-                multiply_projection(*tile_of(turn))
-            if is_item(step):
-                multiply_scores(*item(step))
-            if part == 0 and is_tile(turn - 3):
-                multiply_weights_and_values(*tile_of(turn - 3))
-            if part == 1 and is_tile(turn - 1):
-                flip_weights(*tile_of(turn - 1), 0)
-            if part == 2:
-                if is_head(turn + 4):
-                    flip_queries_and_keys(*head_of(turn + 4))
-                if batch_starting_at(turn + 7) is not None:
-                    flip_nodes(batch_starting_at(turn + 7), 0)
-                if batch_starting_at(turn + 6) is not None:
-                    flip_nodes(batch_starting_at(turn + 6), 1)
-            if part == 3:
-                if is_tile(turn - 1):
-                    flip_weights(*tile_of(turn - 1), 2)
-                if is_head(turn + 3):
-                    multiply_values(*head_of(turn + 3))
+        for i in range(ITEMS):
+            put(i, 11, multiply_scores, *item(i))
+            put(i + 1, 20, scale_and_find_maximum, *item(i))
+            put(i + 2, 30, exponentiate, *item(i))
 
-            if is_item(step - 1):
-                scale_and_find_maximum(*item(step - 1))
-            if part == 0 and is_tile(turn - 4):
-                add_streams(*tile_of(turn - 4))
-                negate_mean(*tile_of(turn - 4))
-            if part == 1 and is_tile(turn - 5):
-                normalise_and_store(*tile_of(turn - 5))
-            if part == 2:
-                if is_tile(turn - 2):
-                    quantise_weights(*tile_of(turn - 2))
-                if is_head(turn + 1):
-                    quantise_values(*head_of(turn + 1))
-                if batch_starting_at(turn + 4) is not None:
-                    quantise_nodes(batch_starting_at(turn + 4))
-            if part == 3:
-                if is_tile(turn):
-                    add_conv_bias(*tile_of(turn))
-                if is_tile(turn - 4):
-                    centre_and_gain(*tile_of(turn - 4))
+        for n in range(TILES):
+            tile = tile_of(n)
+            put(at(n + 1, 1), 12, flip_weights, *tile, 0)
+            put(at(n + 1, 2), 31, keep_weights, *tile, 0)
+            put(at(n + 1, 3), 12, flip_weights, *tile, 2)
+            put(at(n + 2, 0), 31, keep_weights, *tile, 2)
+            put(at(n + 2, 0), 32, invert_row_sums, *tile)
+            put(at(n + 2, 2), 21, quantise_weights, *tile)
+            put(at(n + 3, 0), 12, multiply_weights_and_values, *tile)
+            put(at(n + 3, 1), 32, divide_by_row_sums, *tile)
+            put(at(n + 2, 1), 10, multiply_projection, *tile)
+            put(at(n + 2, 3), 21, add_conv_bias, *tile)
+            put(at(n + 4, 0), 21, add_streams, *tile)
+            put(at(n + 4, 0), 22, negate_mean, *tile)
+            put(at(n + 4, 2), 32, invert_deviation, *tile)
+            put(at(n + 4, 3), 22, centre_and_gain, *tile)
+            put(at(n + 5, 1), 21, normalise_and_store, *tile)
 
-            if is_item(step - 2):
-                exponentiate(*item(step - 2))
-            if part == 0:
-                if is_tile(turn - 2):
-                    keep_weights(*tile_of(turn - 2), 2)
-                    invert_row_sums(*tile_of(turn - 2))
-                if batch_starting_at(turn + 6) is not None:
-                    keep_nodes(batch_starting_at(turn + 6), 0)
-                if batch_starting_at(turn + 5) is not None:
-                    keep_nodes(batch_starting_at(turn + 5), 1)
-            if part == 1:
-                if is_head(turn + 2):
-                    round_values(*head_of(turn + 2))
-                if is_tile(turn - 3):
-                    divide_by_row_sums(*tile_of(turn - 3))
-            if part == 2:
-                if is_tile(turn - 1):
-                    keep_weights(*tile_of(turn - 1), 0)
-                if is_tile(turn - 4):
-                    invert_deviation(*tile_of(turn - 4))
-            if part == 3 and is_head(turn + 4):
-                keep_queries_and_keys(*head_of(turn + 4))
+        for m in range(HEADS):
+            head = head_of(m)
+            if m >= H:
+                put(at(m - 4, 2), 12, flip_queries_and_keys, *head)
+                put(at(m - 4, 3), 31, keep_queries_and_keys, *head)
+            else:
+                put(m - 4, 12, flip_queries_and_keys, *head)
+                put(m - 3, 31, keep_queries_and_keys, *head)
+            if m >= 3:
+                put(at(m - 2, 3), 14, multiply_values, *head)
+                put(at(m - 1, 1), 31, round_values, *head)
+                put(at(m - 1, 2), 22, quantise_values, *head)
+            else:
+                put(5 + m, 14, multiply_values, *head)
+                put(6 + m, 33, round_values, *head)
+                put(at(2, 2), 22, quantise_values, *head)
+
+        for b in range(B):
+            if b >= 2:
+                for h in range(H):
+                    put(at(4 * b - 6, 0), h, load_queries_and_keys, b, h)
+                put(at(4 * b - 6, 0), H, load_nodes, b)
+            if b >= 1:
+                put(at(4 * b - 3, 2), 13, flip_nodes, b, 0)
+                put(at(4 * b - 3, 3), 32, keep_nodes, b, 0)
+                put(at(4 * b - 3, 3), 13, flip_nodes, b, 1)
+                put(at(4 * b - 2, 0), 33, keep_nodes, b, 1)
+                put(at(4 * b - 2, 2), 23, quantise_nodes, b)
+            else:
+                put(0, 13, flip_nodes, b, 0)
+                put(1, 33, keep_nodes, b, 0)
+                put(1, 13, flip_nodes, b, 1)
+                put(2, 33, keep_nodes, b, 1)
+                put(3, 23, quantise_nodes, b)
+
+        put(3, 24, group_value_weights)
+        put(4, 24, quantise_value_weights)
+        for pair in range(2):
+            put(2 + pair, 15, flip_conv_weights, pair)
+            put(3 + pair, 34, keep_conv_weights, pair)
+        put(6, 24, quantise_conv_weights)
+
+        warm = const.tile([P, 2], F32, name="warm")
+        nc.vector.memset(warm[:], 0.0)
+        nc.scalar.activation(out=warm[:, 1:2], in_=warm[:, 0:1], func=ACT.Exp)
+
+        for h in range(H):
+            load_queries_and_keys(0, h)
+        load_nodes(0)
+        load_queries_and_keys(1, 0)
+        load_value_weights()
+        load_conv_weights()
+        load_nodes(1)
+        for h in range(1, H):
+            load_queries_and_keys(1, h)
+        load_channel_vectors()
+
+        for step in sorted(plan):
+            for place, work_of, args in sorted(plan[step], key=lambda entry: entry[0]):
+                work_of(*args)

@@ -126,8 +126,6 @@ def tile_transformergraphconv_pa_t_kernel(
         make_identity(nc, ident_bf16[:])
         minus_half = const.tile([P, 1], F32, name="minus_half")
         nc.vector.memset(minus_half[:], -0.5)
-        minus_one = const.tile([P, H], F32, name="minus_one")
-        nc.vector.memset(minus_one[:], -1.0)
 
         cw_banks, cw_grouped = {}, {}
 
@@ -332,9 +330,7 @@ def tile_transformergraphconv_pa_t_kernel(
 
         def invert_row_sums(b, j):
             inv_sum = small.tile([P, H], F32, name="inv_sum")
-            nc.gpsimd.tensor_tensor(
-                out=inv_sum[:], in0=row_sums[(b, j)][:], in1=minus_one[:], op=ALU.pow
-            )
+            nc.vector.reciprocal(inv_sum[:], row_sums[(b, j)][:])
             inv_sums[(b, j)] = inv_sum
 
         def add_conv_bias(b, j):
@@ -369,17 +365,14 @@ def tile_transformergraphconv_pa_t_kernel(
 
         def negate_mean(b, j):
             neg_mean = small.tile([P, 1], F32, name="neg_mean")
-            nc.gpsimd.tensor_scalar(
-                out=neg_mean[:],
-                in0=y_sums[(b, j)][:],
-                scalar1=-1.0 / C_OUT,
-                scalar2=0.0,
-                op0=ALU.mult,
-                op1=ALU.add,
+            nc.scalar.activation(
+                out=neg_mean[:], in_=y_sums[(b, j)][:], func=ACT.Copy, scale=-1.0 / C_OUT
             )
             neg_means[(b, j)] = neg_mean
 
-        def invert_deviation(b, j):
+        square_sums = {}
+
+        def sum_squares(b, j):
             squares = work.tile([P, C_OUT], BF16, name="squares", bufs=2)
             square_sum = small.tile([P, 1], F32, name="square_sum")
             nc.scalar.activation(
@@ -390,10 +383,13 @@ def tile_transformergraphconv_pa_t_kernel(
                 scale=1.0,
                 accum_out=square_sum[:],
             )
+            square_sums[(b, j)] = square_sum
+
+        def invert_deviation(b, j):
             var_eps = small.tile([P, 1], F32, name="var_eps")
             nc.gpsimd.tensor_scalar(
                 out=var_eps[:],
-                in0=square_sum[:],
+                in0=square_sums[(b, j)][:],
                 scalar1=1.0 / C_OUT,
                 scalar2=LN_EPS,
                 op0=ALU.mult,
@@ -459,15 +455,16 @@ def tile_transformergraphconv_pa_t_kernel(
             put(at(n + 1, 2), 31, keep_weights, *tile, 0)
             put(at(n + 1, 3), 12, flip_weights, *tile, 2)
             put(at(n + 2, 0), 31, keep_weights, *tile, 2)
-            put(at(n + 2, 0), 32, invert_row_sums, *tile)
+            put(at(n + 2, 1), 22, invert_row_sums, *tile)
             put(at(n + 2, 2), 21, quantise_weights, *tile)
             put(at(n + 3, 0), 12, multiply_weights_and_values, *tile)
             put(at(n + 3, 1), 32, divide_by_row_sums, *tile)
             put(at(n + 2, 1), 10, multiply_projection, *tile)
             put(at(n + 2, 3), 21, add_conv_bias, *tile)
             put(at(n + 4, 0), 21, add_streams, *tile)
-            put(at(n + 4, 0), 22, negate_mean, *tile)
-            put(at(n + 4, 2), 32, invert_deviation, *tile)
+            put(at(n + 4, 1), 33, negate_mean, *tile)
+            put(at(n + 4, 2), 32, sum_squares, *tile)
+            put(at(n + 4, 2), 33, invert_deviation, *tile)
             put(at(n + 4, 3), 22, centre_and_gain, *tile)
             put(at(n + 5, 1), 21, normalise_and_store, *tile)
 

@@ -314,6 +314,18 @@ def tile_transformergraphconv_pa_t_kernel(
             )
             projected[(b, j)] = proj
 
+        def repeat_projection(b, j):
+            spare = product_banks.tile([P, C_OUT], F32, name="spare", tag="product")
+            nc.tensor.matmul_mx(
+                out=spare[:],
+                lhsT=x_codes[b][:, tile_cols(j)].bitcast(FP8X4),
+                lhsT_scale=x_scales[b][:, tile_cols(j)],
+                rhs=cw_codes[:].bitcast(FP8X4),
+                rhs_scale=cw_scales[:],
+                start=True,
+                stop=True,
+            )
+
         def multiply_weights_and_values(b, j):
             att = product_banks.tile([P, H, DH], F32, name="att", tag="product")
             for h in range(H):
@@ -461,6 +473,7 @@ def tile_transformergraphconv_pa_t_kernel(
             put(at(n + 3, 1), 32, divide_by_row_sums, *tile)
             put(at(n + 2, 1), 10, multiply_projection, *tile)
             put(at(n + 2, 3), 21, add_conv_bias, *tile)
+            put(at(n + 2, 2), 10, repeat_projection, *tile)
             put(at(n + 4, 0), 21, add_streams, *tile)
             put(at(n + 4, 1), 33, negate_mean, *tile)
             put(at(n + 4, 2), 32, sum_squares, *tile)

@@ -459,7 +459,7 @@ def tile_transformergraphconv_pa_t_kernel(
         for i in range(ITEMS):
             put(i, 11, multiply_scores, *item(i))
             put(i + 1, 20, scale_and_find_maximum, *item(i))
-            put(i + 2, 30, exponentiate, *item(i))
+            put(i + 2, 36, exponentiate, *item(i))
 
         for n in range(TILES):
             tile = tile_of(n)

import math
from contextlib import ExitStack

import concourse.mybir as mybir
from concourse.masks import make_identity

F32 = mybir.dt.float32
BF16 = mybir.dt.bfloat16
U32 = mybir.dt.uint32
U8 = mybir.dt.uint8
FP8X4 = mybir.dt.float8_e4m3fn_x4
ALU = mybir.AluOpType
ACT = mybir.ActivationFunctionType

P = 128
PACK = 4
B, N, C_IN, C_OUT, H = 8, 512, 512, 512, 4
DH = C_OUT // H
NODE_TILES = N // P
LN_EPS = 1e-5
SCORE_SCALE = 1.0 / math.sqrt(DH)

assert C_IN == P * PACK and N == P * PACK
assert DH == P and NODE_TILES == PACK

FLOPS = 2 * B * (N * C_IN * H * DH + N * C_IN * C_OUT + 2 * H * N * N * DH)

ITEMS = B * NODE_TILES * H
TILES = B * NODE_TILES
HEADS = B * H


def tile_transformergraphconv_pa_t_kernel(
    tc, x, q, k, W_v, conv_w, conv_b, ln_w, ln_b, out
):
    nc = tc.nc
    with ExitStack() as ctx:
        ctx.enter_context(tc.manual_schedule())
        const = ctx.enter_context(tc.tile_pool(name="const", bufs=1))
        rows_pool = ctx.enter_context(tc.tile_pool(name="rows", bufs=2))
        batch_pool = ctx.enter_context(tc.tile_pool(name="batch", bufs=3))
        work = ctx.enter_context(tc.tile_pool(name="work", bufs=3))
        small = ctx.enter_context(tc.tile_pool(name="small", bufs=8))
        score_banks = ctx.enter_context(tc.psum_pool(name="score_banks", bufs=2))
        flip_banks = ctx.enter_context(tc.psum_pool(name="flip_banks", bufs=3))
        product_banks = ctx.enter_context(tc.psum_pool(name="product_banks", bufs=3))

        def head_cols(h):
            return slice(h * DH, (h + 1) * DH)

        def tile_cols(j):
            return slice(j * P, (j + 1) * P)

        x_rows, q_rows, k_rows = {}, {}, {}

        def load_queries_and_keys(b, h):
            if h == 0:
                q_tile = rows_pool.tile([P, H, NODE_TILES, DH], BF16, name="q_tile")
                k_tile = rows_pool.tile([P, H, 2, 2, DH], BF16, name="k_tile")
                q_rows[b], k_rows[b] = q_tile, k_tile
            nc.sync.dma_start(
                out=q_rows[b][:, h, :, :].rearrange("p j d -> p (j d)"),
                in_=q[b][h].rearrange("(p j) d -> p (j d)", j=NODE_TILES),
            )
            nc.sync.dma_start(
                out=k_rows[b][:, h, :, :, :].rearrange("p a u d -> p a (u d)"),
                in_=k[b][h].rearrange("(a p u) d -> p a (u d)", a=2, u=2),
            )

        def load_nodes(b):
            x_tile = rows_pool.tile([P, NODE_TILES * C_IN], BF16, name="x_tile")
            nc.sync.dma_start(
                out=x_tile[:], in_=x[b].rearrange("(p j) c -> p (j c)", j=NODE_TILES)
            )
            x_rows[b] = x_tile

        def transpose_channels(rows, pair):
            words = rows.bitcast(F32)
            flipped = flip_banks.tile([P, 2, 2 * P], F32, name="flipped", tag="flip")
            for i in range(2):
                for u in range(2):
                    first_word = (2 * pair + i) * (C_IN // 2) + u * P
                    nc.tensor.transpose(
                        flipped[:, u, tile_cols(i)],
                        words[:, first_word : first_word + P],
                        ident_f32[:],
                    )
            return flipped

        def keep_channels(flipped, grouped, pair):
            grouped_words = grouped[:].bitcast(F32).rearrange("p (c u) -> p c u", u=2)
            nc.scalar.copy(
                out=grouped_words[:, pair * 2 * P : (pair + 1) * 2 * P, :],
                in_=flipped[:].rearrange("p u c -> p c u"),
            )

        cw_rows = const.tile([P, PACK * C_IN], BF16, name="cw_rows")
        wv_rows = const.tile([P, H, PACK, DH], BF16, name="wv_rows")
        bias_all = const.tile([P, C_OUT], BF16, name="bias_all")
        gain_all = const.tile([P, C_OUT], BF16, name="gain_all")
        shift_all = const.tile([P, C_OUT], BF16, name="shift_all")

        def load_value_weights():
            for u in range(2):
                nc.sync.dma_start(
                    out=wv_rows[:, :, 2 * u : 2 * u + 2, :].rearrange("p h i d -> p h (i d)"),
                    in_=W_v[:, u * 2 * P : (u + 1) * 2 * P, :].rearrange(
                        "h (p i) d -> p h (i d)", i=2
                    ),
                )

        def load_conv_weights():
            nc.sync.dma_start(
                out=cw_rows[:].rearrange("p (r c) -> p r c", c=C_IN),
                in_=conv_w.rearrange("(r p) c -> p r c", p=P),
            )

        def load_channel_vectors():
            nc.sync.dma_start(out=bias_all[:], in_=conv_b.partition_broadcast(P))
            nc.sync.dma_start(out=gain_all[:], in_=ln_w.partition_broadcast(P))
            nc.sync.dma_start(out=shift_all[:], in_=ln_b.partition_broadcast(P))

        ident_f32 = const.tile([P, P], F32, name="ident_f32")
        make_identity(nc, ident_f32[:])
        ident_bf16 = const.tile([P, P], BF16, name="ident_bf16")
        make_identity(nc, ident_bf16[:])
        minus_half = const.tile([P, 1], F32, name="minus_half")
        nc.vector.memset(minus_half[:], -0.5)

        cw_banks, cw_grouped = {}, {}

        def flip_conv_weights(pair):
            cw_banks[pair] = transpose_channels(cw_rows[:], pair)

        def keep_conv_weights(pair):
            if pair == 0:
                grouped = work.tile(
                    [P, PACK * P * PACK], BF16, name="grouped", align_bytes=64, bufs=2
                )
                cw_grouped[0] = grouped
            keep_channels(cw_banks[pair], cw_grouped[0], pair)

        def quantise_conv_weights():
            nc.vector.quantize_mx(
                out=cw_codes[:].bitcast(FP8X4), scales=cw_scales[:], in_=cw_grouped[0][:]
            )

        def group_value_weights():
            nc.vector.tensor_copy(out=wv_grouped[:], in_=wv_rows[:].rearrange("p h t d -> p h d t"))

        def quantise_value_weights():
            nc.vector.quantize_mx(
                out=wv_codes[:].bitcast(FP8X4),
                scales=wv_scales[:],
                in_=wv_grouped[:].rearrange("p h d t -> p (h d t)"),
            )

        wv_grouped = const.tile([P, H, DH, PACK], BF16, name="wv_grouped", align_bytes=64)
        cw_codes = const.tile([P, C_OUT], U32, name="cw_codes", align_bytes=64)
        cw_scales = const.tile([P, C_OUT], U8, name="cw_scales", align_bytes=64)
        wv_codes = const.tile([P, H * DH], U32, name="wv_codes", align_bytes=64)
        wv_scales = const.tile([P, H * DH], U8, name="wv_scales", align_bytes=64)

        x_banks, x_grouped, x_codes, x_scales = {}, {}, {}, {}

        def flip_nodes(b, pair):
            x_banks[(b, pair)] = transpose_channels(x_rows[b][:], pair)

        def keep_nodes(b, pair):
            if pair == 0:
                grouped = work.tile(
                    [P, PACK * P * PACK], BF16, name="grouped", align_bytes=64, bufs=2
                )
                x_grouped[b] = grouped
            keep_channels(x_banks[(b, pair)], x_grouped[b], pair)

        def quantise_nodes(b):
            xc = batch_pool.tile([P, N], U32, name="xc", align_bytes=64)
            xs = batch_pool.tile([P, N], U8, name="xs", align_bytes=64)
            nc.vector.quantize_mx(out=xc[:].bitcast(FP8X4), scales=xs[:], in_=x_grouped[b][:])
            x_codes[b], x_scales[b] = xc, xs

        qk_banks, qk_flipped = {}, {}
        value_banks, v_grouped, v_codes, v_scales = {}, {}, {}, {}

        def flip_queries_and_keys(b, h):
            flipped = flip_banks.tile([P, 2, N], BF16, name="flipped", tag="flip")
            for j in range(NODE_TILES):
                nc.tensor.transpose(flipped[:, 0, tile_cols(j)], q_rows[b][:, h, j, :], ident_bf16[:])
            for u in range(2):
                for a in range(2):
                    nc.tensor.transpose(
                        flipped[:, 1, tile_cols(2 * u + a)], k_rows[b][:, h, a, u, :], ident_bf16[:]
                    )
            qk_banks[(b, h)] = flipped

        def keep_queries_and_keys(b, h):
            qk = batch_pool.tile([P, 2, N], BF16, name="qk", bufs=3 * H)
            nc.scalar.copy(out=qk[:], in_=qk_banks[(b, h)][:])
            qk_flipped[(b, h)] = qk

        def multiply_values(b, h):
            values = product_banks.tile([P, PACK, DH], F32, name="values", tag="product")
            for t in range(PACK):
                j = 2 * (t % 2) + t // 2
                nc.tensor.matmul_mx(
                    out=values[:, t, :],
                    lhsT=x_codes[b][:, tile_cols(j)].bitcast(FP8X4),
                    lhsT_scale=x_scales[b][:, tile_cols(j)],
                    rhs=wv_codes[:, head_cols(h)].bitcast(FP8X4),
                    rhs_scale=wv_scales[:, head_cols(h)],
                    start=True,
                    stop=True,
                )
            value_banks[(b, h)] = values

        def round_values(b, h):
            vg = work.tile([P, DH, PACK], BF16, name="vg", align_bytes=64, bufs=4)
            nc.scalar.copy(out=vg[:], in_=value_banks[(b, h)][:].rearrange("p t d -> p d t"))
            v_grouped[(b, h)] = vg

        def quantise_values(b, h):
            vc = batch_pool.tile([P, DH], U32, name="vc", align_bytes=64, bufs=3 * H)
            vs = batch_pool.tile([P, DH], U8, name="vs", align_bytes=64, bufs=3 * H)
            nc.vector.quantize_mx(
                out=vc[:].bitcast(FP8X4),
                scales=vs[:],
                in_=v_grouped[(b, h)][:].rearrange("p d t -> p (d t)"),
            )
            v_codes[(b, h)], v_scales[(b, h)] = vc, vs

        scores, neg_scores, exp_bias, e_rows = {}, {}, {}, {}
        row_sums, e_banks, e_grouped = {}, {}, {}

        def multiply_scores(b, j, h):
            s = score_banks.tile([P, N], F32, name="s", tag="scores")
            nc.tensor.matmul(
                out=s[:],
                lhsT=qk_flipped[(b, h)][:, 0, tile_cols(j)],
                rhs=qk_flipped[(b, h)][:, 1, :],
                start=True,
                stop=True,
            )
            scores[(b, j, h)] = s

        def scale_and_find_maximum(b, j, h):
            ns = work.tile([P, N], F32, name="ns", bufs=6)
            nb = small.tile([P, 1], F32, name="nb")
            nc.vector.tensor_scalar(
                out=ns[:],
                in0=scores[(b, j, h)][:],
                scalar1=-SCORE_SCALE,
                scalar2=None,
                op0=ALU.mult,
                op1=ALU.min,
                accum_out=nb[:],
            )
            neg_scores[(b, j, h)], exp_bias[(b, j, h)] = ns, nb

        def exponentiate(b, j, h):
            if h == 0:
                row_sum = small.tile([P, H], F32, name="row_sum")
                row_sums[(b, j)] = row_sum
            e_item = work.tile([P, N], BF16, name="e_item", bufs=6)
            nc.scalar.activation(
                out=e_item[:],
                in_=neg_scores[(b, j, h)][:],
                func=ACT.Exp,
                bias=exp_bias[(b, j, h)][:],
                scale=-1.0,
                accum_out=row_sums[(b, j)][:, h : h + 1],
            )
            e_rows[(b, j, h)] = e_item

        def flip_weights(b, j, first):
            flipped = flip_banks.tile([P, 2, 2, P], F32, name="flipped", tag="flip")
            for i in range(2):
                words = e_rows[(b, j, first + i)][:].bitcast(F32)
                for u in range(2):
                    nc.tensor.transpose(flipped[:, i, u, :], words[:, tile_cols(u)], ident_f32[:])
            e_banks[(b, j, first)] = flipped

        def keep_weights(b, j, first):
            if first == 0:
                eg = work.tile([P, H * P * PACK], BF16, name="eg", align_bytes=64)
                e_grouped[(b, j)] = eg
            eg_words = e_grouped[(b, j)][:].bitcast(F32).rearrange("p (h n u) -> p h n u", h=H, u=2)
            nc.scalar.copy(
                out=eg_words[:, first : first + 2, :, :],
                in_=e_banks[(b, j, first)][:].rearrange("p i u n -> p i n u"),
            )

        e_codes, e_scales, attended, projected = {}, {}, {}, {}
        inv_sums, conv, mixed, y_tiles, y_sums, neg_means, inv_stds, centred = (
            {}, {}, {}, {}, {}, {}, {}, {},
        )

        def quantise_weights(b, j):
            ec = work.tile([P, H * P], U32, name="ec", align_bytes=64)
            es = work.tile([P, H * P], U8, name="es", align_bytes=64)
            nc.vector.quantize_mx(out=ec[:].bitcast(FP8X4), scales=es[:], in_=e_grouped[(b, j)][:])
            e_codes[(b, j)], e_scales[(b, j)] = ec, es

        def multiply_projection(b, j):
            proj = product_banks.tile([P, C_OUT], F32, name="proj", tag="product")
            nc.tensor.matmul_mx(
                out=proj[:],
                lhsT=x_codes[b][:, tile_cols(j)].bitcast(FP8X4),
                lhsT_scale=x_scales[b][:, tile_cols(j)],
                rhs=cw_codes[:].bitcast(FP8X4),
                rhs_scale=cw_scales[:],
                start=True,
                stop=True,
            )
            projected[(b, j)] = proj

        def repeat_projection(b, j):
            spare = product_banks.tile([P, C_OUT], F32, name="spare", tag="product")
            nc.tensor.matmul_mx(
                out=spare[:],
                lhsT=x_codes[b][:, tile_cols(j)].bitcast(FP8X4),
                lhsT_scale=x_scales[b][:, tile_cols(j)],
                rhs=cw_codes[:].bitcast(FP8X4),
                rhs_scale=cw_scales[:],
                start=True,
                stop=True,
            )

        def multiply_weights_and_values(b, j):
            att = product_banks.tile([P, H, DH], F32, name="att", tag="product")
            for h in range(H):
                nc.tensor.matmul_mx(
                    out=att[:, h, :],
                    lhsT=e_codes[(b, j)][:, tile_cols(h)].bitcast(FP8X4),
                    lhsT_scale=e_scales[(b, j)][:, tile_cols(h)],
                    rhs=v_codes[(b, h)][:].bitcast(FP8X4),
                    rhs_scale=v_scales[(b, h)][:],
                    start=True,
                    stop=True,
                )
            attended[(b, j)] = att

        def invert_row_sums(b, j):
            inv_sum = small.tile([P, H], F32, name="inv_sum")
            nc.vector.reciprocal(inv_sum[:], row_sums[(b, j)][:])
            inv_sums[(b, j)] = inv_sum

        def add_conv_bias(b, j):
            cv = work.tile([P, C_OUT], F32, name="cv", bufs=6)
            nc.vector.tensor_tensor(out=cv[:], in0=projected[(b, j)][:], in1=bias_all[:], op=ALU.add)
            conv[(b, j)] = cv

        def divide_by_row_sums(b, j):
            scaled = work.tile([P, H, DH], F32, name="scaled")
            for h in range(H):
                nc.scalar.activation(
                    out=scaled[:, h, :],
                    in_=attended[(b, j)][:, h, :],
                    func=ACT.Relu,
                    scale=inv_sums[(b, j)][:, h : h + 1],
                )
            mixed[(b, j)] = scaled

        def add_streams(b, j):
            y = work.tile([P, C_OUT], F32, name="y")
            y_sum = small.tile([P, 1], F32, name="y_sum")
            nc.vector.scalar_tensor_tensor(
                out=y[:],
                in0=mixed[(b, j)][:].rearrange("p h d -> p (h d)"),
                scalar=0.0,
                in1=conv[(b, j)][:],
                op0=ALU.max,
                op1=ALU.add,
                accum_out=y_sum[:],
            )
            y_tiles[(b, j)], y_sums[(b, j)] = y, y_sum

        def negate_mean(b, j):
            neg_mean = small.tile([P, 1], F32, name="neg_mean")
            nc.scalar.activation(
                out=neg_mean[:], in_=y_sums[(b, j)][:], func=ACT.Copy, scale=-1.0 / C_OUT
            )
            neg_means[(b, j)] = neg_mean

        square_sums = {}

        def sum_squares(b, j):
            squares = work.tile([P, C_OUT], BF16, name="squares", bufs=2)
            square_sum = small.tile([P, 1], F32, name="square_sum")
            nc.scalar.activation(
                out=squares[:],
                in_=y_tiles[(b, j)][:],
                func=ACT.Square,
                bias=neg_means[(b, j)][:],
                scale=1.0,
                accum_out=square_sum[:],
            )
            square_sums[(b, j)] = square_sum

        def invert_deviation(b, j):
            var_eps = small.tile([P, 1], F32, name="var_eps")
            nc.gpsimd.tensor_scalar(
                out=var_eps[:],
                in0=square_sums[(b, j)][:],
                scalar1=1.0 / C_OUT,
                scalar2=LN_EPS,
                op0=ALU.mult,
                op1=ALU.add,
            )
            inv_std = small.tile([P, 1], F32, name="inv_std")
            nc.gpsimd.tensor_tensor(out=inv_std[:], in0=var_eps[:], in1=minus_half[:], op=ALU.pow)
            inv_stds[(b, j)] = inv_std

        def centre_and_gain(b, j):
            t = work.tile([P, C_OUT], F32, name="t")
            nc.vector.scalar_tensor_tensor(
                out=t[:],
                in0=y_tiles[(b, j)][:],
                scalar=neg_means[(b, j)][:],
                in1=gain_all[:],
                op0=ALU.add,
                op1=ALU.mult,
            )
            centred[(b, j)] = t

        def normalise_and_store(b, j):
            result = work.tile([P, C_OUT], F32, name="result", bufs=4)
            nc.vector.scalar_tensor_tensor(
                out=result[:],
                in0=centred[(b, j)][:],
                scalar=inv_stds[(b, j)][:],
                in1=shift_all[:],
                op0=ALU.mult,
                op1=ALU.add,
            )
            nc.sync.dma_start(
                out=out[b].rearrange("(p j) c -> p j c", j=NODE_TILES)[:, j, :], in_=result[:]
            )

        def item(i):
            b, rest = divmod(i, NODE_TILES * H)
            j, h = divmod(rest, H)
            return b, j, h

        def tile_of(n):
            return divmod(n, NODE_TILES)

        def head_of(m):
            return divmod(m, H)

        plan = {}

        def put(step, place, work_of, *args):
            plan.setdefault(step, []).append((place, work_of, args))

        def at(turn, part):
            return H * turn + part

        for i in range(ITEMS):
            put(i, 11, multiply_scores, *item(i))
            put(i + 1, 20, scale_and_find_maximum, *item(i))
            put(i + 2, 36, exponentiate, *item(i))

        for n in range(TILES):
            tile = tile_of(n)
            put(at(n + 1, 1), 12, flip_weights, *tile, 0)
            put(at(n + 1, 2), 31, keep_weights, *tile, 0)
            put(at(n + 1, 3), 12, flip_weights, *tile, 2)
            put(at(n + 2, 0), 31, keep_weights, *tile, 2)
            put(at(n + 2, 1), 22, invert_row_sums, *tile)
            put(at(n + 2, 2), 21, quantise_weights, *tile)
            put(at(n + 3, 0), 12, multiply_weights_and_values, *tile)
            put(at(n + 3, 1), 32, divide_by_row_sums, *tile)
            put(at(n + 2, 1), 10, multiply_projection, *tile)
            put(at(n + 2, 3), 21, add_conv_bias, *tile)
            put(at(n + 2, 2), 10, repeat_projection, *tile)
            put(at(n + 4, 0), 21, add_streams, *tile)
            put(at(n + 4, 1), 33, negate_mean, *tile)
            put(at(n + 4, 2), 32, sum_squares, *tile)
            put(at(n + 4, 2), 33, invert_deviation, *tile)
            put(at(n + 4, 3), 22, centre_and_gain, *tile)
            put(at(n + 5, 1), 21, normalise_and_store, *tile)

        for m in range(HEADS):
            head = head_of(m)
            if m >= H:
                put(at(m - 4, 2), 12, flip_queries_and_keys, *head)
                put(at(m - 4, 3), 31, keep_queries_and_keys, *head)
            else:
                put(m - 4, 12, flip_queries_and_keys, *head)
                put(m - 3, 31, keep_queries_and_keys, *head)
            if m >= 3:
                put(at(m - 2, 3), 14, multiply_values, *head)
                put(at(m - 1, 1), 31, round_values, *head)
                put(at(m - 1, 2), 22, quantise_values, *head)
            else:
                put(5 + m, 14, multiply_values, *head)
                put(6 + m, 33, round_values, *head)
                put(at(2, 2), 22, quantise_values, *head)

        for b in range(B):
            if b >= 2:
                for h in range(H):
                    put(at(4 * b - 6, 0), h, load_queries_and_keys, b, h)
                put(at(4 * b - 6, 0), H, load_nodes, b)
            if b >= 1:
                put(at(4 * b - 3, 2), 13, flip_nodes, b, 0)
                put(at(4 * b - 3, 3), 32, keep_nodes, b, 0)
                put(at(4 * b - 3, 3), 13, flip_nodes, b, 1)
                put(at(4 * b - 2, 0), 33, keep_nodes, b, 1)
                put(at(4 * b - 2, 2), 23, quantise_nodes, b)
            else:
                put(0, 13, flip_nodes, b, 0)
                put(1, 33, keep_nodes, b, 0)
                put(1, 13, flip_nodes, b, 1)
                put(2, 33, keep_nodes, b, 1)
                put(3, 23, quantise_nodes, b)

        put(3, 24, group_value_weights)
        put(4, 24, quantise_value_weights)
        for pair in range(2):
            put(2 + pair, 15, flip_conv_weights, pair)
            put(3 + pair, 34, keep_conv_weights, pair)
        put(6, 24, quantise_conv_weights)

        warm = const.tile([P, 2], F32, name="warm")
        nc.vector.memset(warm[:], 0.0)
        nc.scalar.activation(out=warm[:, 1:2], in_=warm[:, 0:1], func=ACT.Exp)

        for h in range(H):
            load_queries_and_keys(0, h)
        load_nodes(0)
        load_queries_and_keys(1, 0)
        load_value_weights()
        load_conv_weights()
        load_nodes(1)
        for h in range(1, H):
            load_queries_and_keys(1, h)
        load_channel_vectors()

        for step in sorted(plan):
            for place, work_of, args in sorted(plan[step], key=lambda entry: entry[0]):
                work_of(*args)
